import numpy as np
import ml_dtypes


def mxq(x, axis, fmt="e4m3"):
    dtype, down = {"e4m3": (ml_dtypes.float8_e4m3fn, 7), "e5m2": (ml_dtypes.float8_e5m2, 14)}[fmt]
    v = np.moveaxis(np.asarray(x, np.float32).astype(ml_dtypes.bfloat16).astype(np.float64), axis, -1)
    blocks = v.reshape(v.shape[:-1] + (-1, 32))
    amax = np.abs(blocks).max(-1, keepdims=True)
    byte = np.maximum(np.where(amax > 0, np.frexp(amax)[1] - 1 + 127, 0) - down, 1)
    scale = np.exp2(byte - 127.0)
    codes = (blocks / scale).astype(np.float32).astype(dtype).astype(np.float64)
    return np.moveaxis((codes * scale).reshape(v.shape), -1, axis)


WIDE = False


def mx_kscale(k):
    if not WIDE:
        return np.ones(k)
    levels = np.array([10, -10, 5, -5, 0])
    a = np.random.permutation(np.resize(levels, k // 512 * 4)).reshape(k // 512, 4)
    idx = np.arange(k)
    return np.exp2(a[idx // 512, idx % 128 // 32])


BF16 = ml_dtypes.bfloat16


def bf(x):
    return np.asarray(x, np.float32).astype(BF16)


def f64(x):
    return np.asarray(x).astype(np.float64)


B, C, H, W = 2, 512, 16, 512

TEMPERATURE = 1.0
DISP_CLAMP = 0.1
SIG = np.sqrt(2.0)


def setup_inputs():
    s = mx_kscale(C)[None, :, None, None]
    return {"img1": bf(np.random.standard_normal((B, C, H, W)) * SIG * s),
            "img2": bf(np.random.standard_normal((B, C, H, W)) * SIG / s),
            "intri1": bf(np.random.uniform(0.5, 1.5, (B, 3, 3))),
            "intri2": bf(np.random.uniform(0.5, 1.5, (B, 3, 3))),
            "extri1": bf(np.random.uniform(0.0, 1.0, (B, 4, 4))),
            "extri2": bf(np.random.uniform(0.5, 1.5, (B, 4, 4)))}


def reference(img1, img2, intri1, intri2, extri1, extri2):
    a = mxq(f64(img1), 1, "e4m3").transpose(0, 2, 3, 1)
    b = mxq(f64(img2), 1, "e4m3").transpose(0, 2, 1, 3)
    vol = (a @ b) / np.sqrt(C)
    idx = np.arange(W) * 1.0
    tril = np.where(idx[None, :] <= idx[:, None], 1.0, 0.0)
    z = vol / TEMPERATURE
    e = np.exp(z - z.max(-1, keepdims=True))
    prob = e / e.sum(-1, keepdims=True) * tril
    corresp = np.sum(prob * idx, axis=-1)[:, None]
    confidence = np.max(prob, axis=-1)[:, None]
    disp = np.abs(corresp - idx) / W
    disp = np.maximum(disp, DISP_CLAMP)
    fx = f64(intri1)[:, 0, 0][:, None, None, None]
    d = f64(extri1)[:, :3, 3] - f64(extri2)[:, :3, 3]
    baseline = np.sqrt(np.sum(d * d, axis=-1))[:, None, None, None]
    depth = fx * baseline / disp
    return depth, confidence

@@ -1,0 +1,405 @@
+from contextlib import ExitStack
+import math
+
+import concourse.bass as bass
+import concourse.mybir as mybir
+import concourse.tile as tile
+from concourse.masks import make_identity
+
+F32 = mybir.dt.float32
+BF16 = mybir.dt.bfloat16
+I32 = mybir.dt.int32
+U32 = mybir.dt.uint32
+U8 = mybir.dt.uint8
+FP8X4 = mybir.dt.float8_e4m3fn_x4
+ALU = mybir.AluOpType
+ACT = mybir.ActivationFunctionType
+AX = mybir.AxisListType
+
+B, C, H, W = 2, 512, 16, 512
+P = 128
+PACK = 4
+NT = W // P
+N_UNITS = B * H
+QUAD = 32
+NK = W // QUAD
+NQD = P // QUAD
+LOOKAHEAD = 5
+SCALE = 1.0 / math.sqrt(C)
+BIG = 3.0e38
+FLOPS = 2 * B * H * W * W * C
+
+CV = 224
+HEAD = [680, 512]
+CG = 0
+PIN = True
+
+
+def tile_costvolume_kernel(tc, img1, img2, intri1, intri2, extri1, extri2, out_0, out_1):
+    nc = tc.nc
+    with ExitStack() as ctx:
+        const = ctx.enter_context(tc.tile_pool(name="const", bufs=1))
+        rawp = ctx.enter_context(tc.tile_pool(name="rawp", bufs=LOOKAHEAD + 1))
+        grpp = ctx.enter_context(tc.tile_pool(name="grpp", bufs=4))
+        qp = ctx.enter_context(tc.tile_pool(name="qp", bufs=3))
+        ep = ctx.enter_context(tc.tile_pool(name="ep", bufs=3))
+        dmp = ctx.enter_context(tc.tile_pool(name="dmp", bufs=1))
+        psum = ctx.enter_context(tc.psum_pool(name="psum", bufs=8))
+        if PIN:
+            ctx.enter_context(tc.manual_schedule())
+
+        views = [im.rearrange("b (p j) h w -> b p j h w", j=PACK) for im in (img1, img2)]
+        raw = {}
+        grouped = {}
+        codes = {}
+        scales = {}
+        banks = {}
+        etile = {}
+        dmt = {}
+
+        def load(q):
+            for g in (0, 1):
+                r = rawp.tile([P, PACK, W], BF16, tag="raw%d" % g, name="raw%d_%d" % (g, q))
+                nc.sync.dma_start(out=r[:], in_=views[g][q // H, :, :, q % H, :])
+                raw[(g, q)] = r
+
+        for q in range(LOOKAHEAD):
+            load(q)
+
+        in1 = const.tile([P, 18], BF16, name="in1")
+        ex1 = const.tile([P, 32], BF16, name="ex1")
+        ex2 = const.tile([P, 32], BF16, name="ex2")
+        nc.scalar.dma_start(out=in1[:], in_=intri1.rearrange("b r c -> (b r c)").partition_broadcast(P))
+        nc.scalar.dma_start(out=ex1[:], in_=extri1.rearrange("b r c -> (b r c)").partition_broadcast(P))
+        nc.scalar.dma_start(out=ex2[:], in_=extri2.rearrange("b r c -> (b r c)").partition_broadcast(P))
+
+        warm = const.tile([P, 1], F32, name="warm")
+        warm2 = const.tile([P, 1], F32, name="warm2")
+        nc.vector.memset(warm[:], 0.0)
+        nc.scalar.activation(out=warm2[:], in_=warm[:], func=ACT.Exp)
+
+        idx_i = const.tile([P, W], I32, name="idx_i")
+        idx_f = const.tile([P, W], F32, name="idx_f")
+        w1_i = const.tile([P, P], I32, name="w1_i")
+        w1_f = const.tile([P, P], F32, name="w1_f")
+        nc.gpsimd.iota(idx_i[:], pattern=[[1, W]], base=0, channel_multiplier=0)
+        nc.gpsimd.iota(w1_i[:], pattern=[[0, N_UNITS], [P, NT]], base=0, channel_multiplier=1)
+        nc.vector.tensor_copy(out=idx_f[:], in_=idx_i[:])
+        nc.vector.tensor_copy(out=w1_f[:], in_=w1_i[:])
+        offs = [P * t * (t + 1) // 2 for t in range(NT)]
+        wtab = const.tile([P, P * NT * (NT + 1) // 2], F32, name="wtab")
+        for t in range(NT):
+            n = P * (t + 1)
+            nc.gpsimd.affine_select(
+                out=wtab[:, offs[t] : offs[t] + n],
+                in_=idx_f[:, 0:n],
+                pattern=[[-1, n]],
+                compare_op=ALU.is_ge,
+                fill=0.0,
+                base=P * t,
+                channel_multiplier=1,
+            )
+        ident = const.tile([P, P], F32, name="ident")
+        make_identity(nc, ident[:])
+        bigt = const.tile([P, NT * NK], F32, name="bigt")
+        cap = const.tile([P, NT * NK], F32, name="cap")
+        nc.vector.memset(bigt[:], BIG)
+        nc.gpsimd.affine_select(
+            out=cap[:],
+            in_=bigt[:],
+            pattern=[[P, NT], [-QUAD, NK]],
+            compare_op=ALU.is_ge,
+            fill=-BIG,
+            base=-QUAD,
+            channel_multiplier=1,
+        )
+        ones = const.tile([P, QUAD], F32, name="ones")
+        tril = const.tile([P, QUAD], F32, name="tril")
+        nc.vector.memset(ones[:], 1.0)
+        for qd in range(NQD):
+            nc.gpsimd.affine_select(
+                out=tril[QUAD * qd : QUAD * (qd + 1), :],
+                in_=ones[QUAD * qd : QUAD * (qd + 1), :],
+                pattern=[[-1, QUAD]],
+                compare_op=ALU.is_ge,
+                fill=0.0,
+                base=0,
+                channel_multiplier=1,
+            )
+        half = const.tile([P, B], F32, name="half")
+        nc.gpsimd.memset(half[:], 0.5)
+
+        bm_all = const.tile([P, N_UNITS * NT * NK], F32, name="bm_all")
+        m_all = const.tile([P, N_UNITS * NT], F32, name="m_all")
+        bias_all = const.tile([P, N_UNITS * NT], F32, name="bias_all")
+        sums = const.tile([P, N_UNITS * NT], F32, name="sums")
+        num_all = const.tile([P, N_UNITS * NT], F32, name="num_all")
+        dmax_all = const.tile([P, N_UNITS * NT], F32, name="dmax_all")
+        junk = [const.tile([P, P * NT * (NT + 1) // 2], F32, name="junk%d" % k) for k in range(2)]
+
+        def regroup_part(kind, u, lo, hi):
+            for g in (0, 1):
+                a = max(lo, W * g) - W * g
+                z = min(hi, W * (g + 1)) - W * g
+                if a >= z:
+                    continue
+                src = raw[(g, u)][:, :, a:z].rearrange("p t (c i) -> p c t i", i=4)
+                dst = grouped[u][:, g, a:z, :].rearrange("p (c i) t -> p c t i", i=4)
+                if kind == "v":
+                    nc.vector.tensor_copy(out=dst, in_=src)
+                elif kind == "s":
+                    nc.scalar.copy(out=dst, in_=src)
+                else:
+                    nc.gpsimd.tensor_scalar(out=dst, in0=src, scalar1=1.0, scalar2=0.0, op0=ALU.mult, op1=ALU.add)
+
+        def regroup(u):
+            grouped[u] = grpp.tile([P, 2, W, PACK], BF16, tag="grouped", name="grouped_%d" % u, align_bytes=64)
+            cv = HEAD[u] if u < len(HEAD) else CV
+            cg = 0 if u < len(HEAD) else CG
+            regroup_part("v", u, 0, cv)
+            regroup_part("g", u, cv, cv + cg)
+            regroup_part("s", u, cv + cg, 2 * W)
+
+        def quantise(u):
+            codes[u] = qp.tile([P, 2 * W], U32, tag="codes", name="codes_%d" % u, align_bytes=64)
+            scales[u] = qp.tile([P, 2 * W], U8, tag="scales", name="scales_%d" % u, align_bytes=64)
+            nc.vector.quantize_mx(
+                out=codes[u][:].bitcast(FP8X4),
+                scales=scales[u][:],
+                in_=grouped[u][:].rearrange("p g w j -> p (g w j)"),
+            )
+
+        def multiply(u):
+            for t in range(NT):
+                bank = psum.tile([P, W], F32, tag="bank", name="bank_%d_%d" % (u, t))
+                banks[(u, t)] = bank
+                nc.tensor.matmul_mx(
+                    out=bank[:],
+                    lhsT=codes[u][:, P * t : P * (t + 1)].bitcast(FP8X4),
+                    lhsT_scale=scales[u][:, P * t : P * (t + 1)],
+                    rhs=codes[u][:, W : 2 * W].bitcast(FP8X4),
+                    rhs_scale=scales[u][:, W : 2 * W],
+                    start=True,
+                    stop=True,
+                )
+
+        def row_max(u):
+            for t in range(NT):
+                c0 = NT * NK * u + NK * t
+                nc.vector.tensor_reduce(
+                    out=bm_all[:, c0 : c0 + NK],
+                    in_=banks[(u, t)][:].rearrange("p (k r) -> p k r", r=QUAD),
+                    axis=AX.X,
+                    op=ALU.max,
+                )
+
+        def row_max_all(u):
+            nc.vector.tensor_reduce(
+                out=m_all[:, NT * u : NT * (u + 1)],
+                in_=bm_all[:, NT * NK * u : NT * NK * (u + 1)].rearrange("p (t k) -> p t k", k=NK),
+                axis=AX.X,
+                op=ALU.max,
+            )
+
+        def exponentials(u):
+            nc.scalar.mul(out=bias_all[:, NT * u : NT * (u + 1)], in_=m_all[:, NT * u : NT * (u + 1)], mul=-SCALE)
+            etile[u] = ep.tile([P, NT * (W + P)], F32, tag="e", name="e_%d" % u)
+            for t in range(NT):
+                col = NT * u + t
+                nc.scalar.activation(
+                    out=etile[u][:, W * t : W * (t + 1)],
+                    in_=banks[(u, t)][:],
+                    func=ACT.Exp,
+                    bias=bias_all[:, col : col + 1],
+                    scale=SCALE,
+                    accum_out=sums[:, col : col + 1],
+                )
+
+        def mask_diag(u):
+            dmt[u] = dmp.tile([P, NT, QUAD], F32, tag="dm", name="dm_%d" % u)
+            for qd in range(NQD):
+                rows = slice(QUAD * qd, QUAD * (qd + 1))
+                nc.gpsimd.tensor_tensor(
+                    out=dmt[u][rows, :, :],
+                    in0=etile[u][rows, :].rearrange("p (t s) -> p t s", s=W + P)[:, :, QUAD * qd : QUAD * (qd + 1)],
+                    in1=tril[rows, :].unsqueeze(1).to_broadcast([QUAD, NT, QUAD]),
+                    op=ALU.mult,
+                )
+
+        def weighted_sums(u, tiles):
+            for t in tiles:
+                n = P * (t + 1)
+                col = NT * u + t
+                nc.vector.scalar_tensor_tensor(
+                    out=junk[u % 2][:, offs[t] : offs[t] + n],
+                    in0=etile[u][:, W * t : W * t + n],
+                    scalar=1.0,
+                    in1=wtab[:, offs[t] : offs[t] + n],
+                    op0=ALU.mult,
+                    op1=ALU.mult,
+                    accum_out=num_all[:, col : col + 1],
+                )
+
+        def diag_max(u):
+            nc.vector.tensor_reduce(out=dmax_all[:, NT * u : NT * (u + 1)], in_=dmt[u][:], axis=AX.X, op=ALU.max)
+
+        def camera_a():
+            dd = const.tile([P, 32], F32, name="dd")
+            nc.vector.tensor_tensor(out=dd[:], in0=ex1[:], in1=ex2[:], op=ALU.subtract)
+            dv = dd[:].rearrange("p (b r c) -> p b r c", b=B, r=4)[:, :, 0:3, 3]
+            sq = const.tile([P, B, 3], F32, name="sq")
+            nc.vector.tensor_tensor(out=sq[:], in0=dv, in1=dv, op=ALU.mult)
+            ss = const.tile([P, B], F32, name="ss")
+            nc.vector.tensor_reduce(out=ss[:], in_=sq[:], axis=AX.X, op=ALU.add)
+            base = const.tile([P, B], F32, name="base")
+            nc.gpsimd.tensor_tensor(out=base[:], in0=ss[:], in1=half[:], op=ALU.pow)
+            fx = const.tile([P, B], F32, name="fx")
+            nc.vector.tensor_copy(out=fx[:], in_=in1[:].rearrange("p (b k) -> p b k", b=B)[:, :, 0])
+            return base, fx
+
+        def camera_b(base, fx):
+            prod = const.tile([P, B], F32, name="kk")
+            nc.vector.tensor_tensor(out=prod[:], in0=base[:], in1=fx[:], op=ALU.mult)
+            return prod
+
+        kk = None
+        cam = None
+        NC = N_UNITS * NT
+        hc = NC // B
+        hu = N_UNITS // B
+        pmm = const.tile([P, N_UNITS, NT * NK], F32, name="pmm")
+        pm = const.tile([P, NC], F32, name="pm")
+        arg = const.tile([P, NC], F32, name="arg")
+        pe = const.tile([P, NC], F32, name="pe")
+        rs = const.tile([P, NC], F32, name="rs")
+        cor = const.tile([P, NC], F32, name="cor")
+        df = const.tile([P, NC], F32, name="df")
+        ab = const.tile([P, NC], F32, name="ab")
+        disp = const.tile([P, NC], F32, name="disp")
+        rd = const.tile([P, NC], F32, name="rd")
+        depth = const.tile([P, NC], F32, name="depth")
+        cn = const.tile([P, NC], F32, name="cn")
+        conf = const.tile([P, NC], F32, name="conf")
+
+        def cols(b):
+            return slice(hc * b, hc * (b + 1))
+
+        def f_pmm(t):
+            n = NQD * (t + 1)
+            nc.vector.tensor_tensor(
+                out=pmm[:].rearrange("p u (t k) -> p u t k", k=NK)[:, :, t, 0:n],
+                in0=bm_all[:].rearrange("p (u t k) -> p u t k", t=NT, k=NK)[:, :, t, 0:n],
+                in1=cap[:, NK * t : NK * t + n].unsqueeze(1).to_broadcast([P, N_UNITS, n]),
+                op=ALU.min,
+            )
+
+        def f_pm(t):
+            n = NQD * (t + 1)
+            nc.vector.tensor_reduce(
+                out=pm[:].rearrange("p (u t) -> p u t", t=NT)[:, :, t],
+                in_=pmm[:].rearrange("p u (t k) -> p u t k", k=NK)[:, :, t, 0:n],
+                axis=AX.X,
+                op=ALU.max,
+            )
+
+        def f_rs(b):
+            nc.vector.reciprocal(out=rs[:, cols(b)], in_=sums[:, cols(b)])
+
+        def f_cor(b):
+            nc.vector.tensor_tensor(out=cor[:, cols(b)], in0=num_all[:, cols(b)], in1=rs[:, cols(b)], op=ALU.mult)
+
+        def f_df(b):
+            nc.vector.tensor_tensor(out=df[:, cols(b)], in0=cor[:, cols(b)], in1=w1_f[:, cols(b)], op=ALU.subtract)
+
+        def f_ab(b):
+            nc.vector.scalar_tensor_tensor(
+                out=ab[:, cols(b)], in0=df[:, cols(b)], scalar=-1.0, in1=df[:, cols(b)], op0=ALU.mult, op1=ALU.max
+            )
+
+        def f_disp(b):
+            nc.vector.tensor_scalar(
+                out=disp[:, cols(b)], in0=ab[:, cols(b)], scalar1=1.0 / W, scalar2=0.1, op0=ALU.mult, op1=ALU.max
+            )
+
+        def f_rd(b):
+            nc.vector.reciprocal(out=rd[:, cols(b)], in_=disp[:, cols(b)])
+
+        def f_depth(b):
+            nc.vector.tensor_scalar(
+                out=depth[:, cols(b)], in0=rd[:, cols(b)], scalar1=kk[:, b : b + 1], scalar2=None, op0=ALU.mult
+            )
+
+        def f_cn(b):
+            nc.vector.tensor_tensor(out=cn[:, cols(b)], in0=pe[:, cols(b)], in1=dmax_all[:, cols(b)], op=ALU.max)
+
+        def f_conf(b):
+            nc.vector.tensor_tensor(out=conf[:, cols(b)], in0=cn[:, cols(b)], in1=rs[:, cols(b)], op=ALU.mult)
+
+        for i in range(-3, N_UNITS + 2):
+            r = i + 3
+            if r + LOOKAHEAD < N_UNITS:
+                load(r + LOOKAHEAD)
+            if 0 <= i + 1 < N_UNITS:
+                quantise(i + 1)
+                multiply(i + 1)
+            if 0 <= i - 2 < N_UNITS:
+                diag_max(i - 2)
+            if 0 <= i < N_UNITS:
+                row_max(i)
+            if i == N_UNITS:
+                f_pmm(3)
+                f_rs(0)
+                f_pmm(2)
+                f_cor(0)
+                f_pm(3)
+                f_df(0)
+                f_pmm(1)
+                f_ab(0)
+                f_pm(2)
+                f_disp(0)
+                f_pmm(0)
+                f_rd(0)
+                f_pm(1)
+                f_depth(0)
+                f_pm(0)
+                nc.vector.scalar_tensor_tensor(
+                    out=arg[:], in0=pm[:], scalar=SCALE, in1=bias_all[:], op0=ALU.mult, op1=ALU.add
+                )
+                nc.scalar.activation(out=pe[:], in_=arg[:], func=ACT.Exp)
+            if 0 <= i - 1 < N_UNITS:
+                weighted_sums(i - 1, [0] if i == N_UNITS else [NT - 1])
+            if 0 <= i < N_UNITS:
+                row_max_all(i)
+                exponentials(i)
+            if r < N_UNITS:
+                regroup(r)
+            if 0 <= i - 1 < N_UNITS:
+                mask_diag(i - 1)
+                weighted_sums(i - 1, [1, 2, 3] if i == N_UNITS else [0, 1, 2])
+            if i == 4:
+                cam = camera_a()
+            if i == 6:
+                kk = camera_b(cam[0], cam[1])
+
+        f_rs(1)
+        f_cn(0)
+        f_cor(1)
+        f_conf(0)
+        f_df(1)
+        f_cn(1)
+        f_ab(1)
+        f_conf(1)
+        f_disp(1)
+        f_rd(1)
+        f_depth(1)
+
+        pt0 = psum.tile([P, W], F32, tag="bank", name="pt0")
+        pt1 = psum.tile([P, W], F32, tag="bank", name="pt1")
+        o0 = const.tile([P, P], F32, name="o0")
+        o1 = const.tile([P, P], F32, name="o1")
+        nc.tensor.transpose(out=pt1[:, 0:P], in_=conf[:], identity=ident[:])
+        nc.scalar.copy(out=o1[:], in_=pt1[:, 0:P])
+        nc.scalar.dma_start(out=out_1.rearrange("b o h (t p) -> (b o h t) p", p=P), in_=o1[:])
+        nc.tensor.transpose(out=pt0[:, 0:P], in_=depth[:], identity=ident[:])
+        nc.scalar.copy(out=o0[:], in_=pt0[:, 0:P])
+        nc.sync.dma_start(out=out_0.rearrange("b o h (t p) -> (b o h t) p", p=P), in_=o0[:])

@@ -29,10 +29,12 @@ SCALE = 1.0 / math.sqrt(C)
 BIG = 3.0e38
 FLOPS = 2 * B * H * W * W * C
 
-CV = 224
+CV = 0
 HEAD = [680, 512]
-CG = 0
+CG = 288
 PIN = True
+AHEAD = 4
+BATCH = 4
 
 
 def tile_costvolume_kernel(tc, img1, img2, intri1, intri2, extri1, extri2, out_0, out_1):
@@ -40,10 +42,9 @@ def tile_costvolume_kernel(tc, img1, img2, intri1, intri2, extri1, extri2, out_0
     with ExitStack() as ctx:
         const = ctx.enter_context(tc.tile_pool(name="const", bufs=1))
         rawp = ctx.enter_context(tc.tile_pool(name="rawp", bufs=LOOKAHEAD + 1))
-        grpp = ctx.enter_context(tc.tile_pool(name="grpp", bufs=4))
+        grpp = ctx.enter_context(tc.tile_pool(name="grpp", bufs=3))
         qp = ctx.enter_context(tc.tile_pool(name="qp", bufs=3))
         ep = ctx.enter_context(tc.tile_pool(name="ep", bufs=3))
-        dmp = ctx.enter_context(tc.tile_pool(name="dmp", bufs=1))
         psum = ctx.enter_context(tc.psum_pool(name="psum", bufs=8))
         if PIN:
             ctx.enter_context(tc.manual_schedule())
@@ -55,7 +56,6 @@ def tile_costvolume_kernel(tc, img1, img2, intri1, intri2, extri1, extri2, out_0
         scales = {}
         banks = {}
         etile = {}
-        dmt = {}
 
         def load(q):
             for g in (0, 1):
@@ -135,6 +135,8 @@ def tile_costvolume_kernel(tc, img1, img2, intri1, intri2, extri1, extri2, out_0
         sums = const.tile([P, N_UNITS * NT], F32, name="sums")
         num_all = const.tile([P, N_UNITS * NT], F32, name="num_all")
         dmax_all = const.tile([P, N_UNITS * NT], F32, name="dmax_all")
+        draw_all = const.tile([P, N_UNITS, NT, QUAD], F32, name="draw_all")
+        dm_all = const.tile([P, N_UNITS, NT, QUAD], F32, name="dm_all")
         junk = [const.tile([P, P * NT * (NT + 1) // 2], F32, name="junk%d" % k) for k in range(2)]
 
         def regroup_part(kind, u, lo, hi):
@@ -145,6 +147,9 @@ def tile_costvolume_kernel(tc, img1, img2, intri1, intri2, extri1, extri2, out_0
                     continue
                 src = raw[(g, u)][:, :, a:z].rearrange("p t (c i) -> p c t i", i=4)
                 dst = grouped[u][:, g, a:z, :].rearrange("p (c i) t -> p c t i", i=4)
+                if kind == "g":
+                    src = raw[(g, u)][:, :, a:z].rearrange("p t w -> p w t")
+                    dst = grouped[u][:, g, a:z, :]
                 if kind == "v":
                     nc.vector.tensor_copy(out=dst, in_=src)
                 elif kind == "s":
@@ -156,9 +161,9 @@ def tile_costvolume_kernel(tc, img1, img2, intri1, intri2, extri1, extri2, out_0
             grouped[u] = grpp.tile([P, 2, W, PACK], BF16, tag="grouped", name="grouped_%d" % u, align_bytes=64)
             cv = HEAD[u] if u < len(HEAD) else CV
             cg = 0 if u < len(HEAD) else CG
-            regroup_part("v", u, 0, cv)
-            regroup_part("g", u, cv, cv + cg)
-            regroup_part("s", u, cv + cg, 2 * W)
+            regroup_part("g", u, 0, cg)
+            regroup_part("v", u, cg, cg + cv)
+            regroup_part("s", u, cg + cv, 2 * W)
 
         def quantise(u):
             codes[u] = qp.tile([P, 2 * W], U32, tag="codes", name="codes_%d" % u, align_bytes=64)
@@ -215,16 +220,21 @@ def tile_costvolume_kernel(tc, img1, img2, intri1, intri2, extri1, extri2, out_0
                     accum_out=sums[:, col : col + 1],
                 )
 
-        def mask_diag(u):
-            dmt[u] = dmp.tile([P, NT, QUAD], F32, tag="dm", name="dm_%d" % u)
+        def realign(u):
             for qd in range(NQD):
                 rows = slice(QUAD * qd, QUAD * (qd + 1))
-                nc.gpsimd.tensor_tensor(
-                    out=dmt[u][rows, :, :],
-                    in0=etile[u][rows, :].rearrange("p (t s) -> p t s", s=W + P)[:, :, QUAD * qd : QUAD * (qd + 1)],
-                    in1=tril[rows, :].unsqueeze(1).to_broadcast([QUAD, NT, QUAD]),
-                    op=ALU.mult,
+                nc.sync.dma_start(
+                    out=draw_all[rows, u, :, :],
+                    in_=etile[u][rows, :].rearrange("p (t s) -> p t s", s=W + P)[:, :, QUAD * qd : QUAD * (qd + 1)],
                 )
+
+        def mask_diag(u):
+            nc.gpsimd.tensor_tensor(
+                out=dm_all[:, u, :, :],
+                in0=draw_all[:, u, :, :],
+                in1=tril[:].unsqueeze(1).to_broadcast([P, NT, QUAD]),
+                op=ALU.mult,
+            )
 
         def weighted_sums(u, tiles):
             for t in tiles:
@@ -240,8 +250,13 @@ def tile_costvolume_kernel(tc, img1, img2, intri1, intri2, extri1, extri2, out_0
                     accum_out=num_all[:, col : col + 1],
                 )
 
-        def diag_max(u):
-            nc.vector.tensor_reduce(out=dmax_all[:, NT * u : NT * (u + 1)], in_=dmt[u][:], axis=AX.X, op=ALU.max)
+        def diag_max(k):
+            nc.vector.tensor_reduce(
+                out=dmax_all[:, NT * BATCH * k : NT * BATCH * (k + 1)],
+                in_=dm_all[:, BATCH * k : BATCH * (k + 1), :, :].rearrange("p u t r -> p (u t) r"),
+                axis=AX.X,
+                op=ALU.max,
+            )
 
         def camera_a():
             dd = const.tile([P, 32], F32, name="dd")
@@ -335,15 +350,15 @@ def tile_costvolume_kernel(tc, img1, img2, intri1, intri2, extri1, extri2, out_0
         def f_conf(b):
             nc.vector.tensor_tensor(out=conf[:, cols(b)], in0=cn[:, cols(b)], in1=rs[:, cols(b)], op=ALU.mult)
 
-        for i in range(-3, N_UNITS + 2):
-            r = i + 3
+        for i in range(-AHEAD, N_UNITS + 2):
+            r = i + AHEAD
             if r + LOOKAHEAD < N_UNITS:
                 load(r + LOOKAHEAD)
             if 0 <= i + 1 < N_UNITS:
                 quantise(i + 1)
                 multiply(i + 1)
-            if 0 <= i - 2 < N_UNITS:
-                diag_max(i - 2)
+            if 0 <= i - 3 < N_UNITS and (i - 3) % BATCH == BATCH - 1:
+                diag_max((i - 3) // BATCH)
             if 0 <= i < N_UNITS:
                 row_max(i)
             if i == N_UNITS:
@@ -374,7 +389,10 @@ def tile_costvolume_kernel(tc, img1, img2, intri1, intri2, extri1, extri2, out_0
             if r < N_UNITS:
                 regroup(r)
             if 0 <= i - 1 < N_UNITS:
-                mask_diag(i - 1)
+                realign(i - 1)
+            if 0 <= i - 2 < N_UNITS:
+                mask_diag(i - 2)
+            if 0 <= i - 1 < N_UNITS:
                 weighted_sums(i - 1, [1, 2, 3] if i == N_UNITS else [0, 1, 2])
             if i == 4:
                 cam = camera_a()
@@ -386,6 +404,7 @@ def tile_costvolume_kernel(tc, img1, img2, intri1, intri2, extri1, extri2, out_0
         f_cor(1)
         f_conf(0)
         f_df(1)
+        diag_max(N_UNITS // BATCH - 1)
         f_cn(1)
         f_ab(1)
         f_conf(1)

@@ -35,6 +35,7 @@ CG = 288
 PIN = True
 AHEAD = 4
 BATCH = 4
+PW = 192
 
 
 def tile_costvolume_kernel(tc, img1, img2, intri1, intri2, extri1, extri2, out_0, out_1):
@@ -45,7 +46,8 @@ def tile_costvolume_kernel(tc, img1, img2, intri1, intri2, extri1, extri2, out_0
         grpp = ctx.enter_context(tc.tile_pool(name="grpp", bufs=3))
         qp = ctx.enter_context(tc.tile_pool(name="qp", bufs=3))
         ep = ctx.enter_context(tc.tile_pool(name="ep", bufs=3))
-        psum = ctx.enter_context(tc.psum_pool(name="psum", bufs=8))
+        psum = ctx.enter_context(tc.psum_pool(name="psum", bufs=7))
+        psp = ctx.enter_context(tc.psum_pool(name="psp", bufs=1))
         if PIN:
             ctx.enter_context(tc.manual_schedule())
 
@@ -56,6 +58,7 @@ def tile_costvolume_kernel(tc, img1, img2, intri1, intri2, extri1, extri2, out_0
         scales = {}
         banks = {}
         etile = {}
+        passed = {}
 
         def load(q):
             for g in (0, 1):
@@ -78,6 +81,8 @@ def tile_costvolume_kernel(tc, img1, img2, intri1, intri2, extri1, extri2, out_0
         nc.vector.memset(warm[:], 0.0)
         nc.scalar.activation(out=warm2[:], in_=warm[:], func=ACT.Exp)
 
+        ident_bf = const.tile([P, P], BF16, name="ident_bf")
+        make_identity(nc, ident_bf[:])
         idx_i = const.tile([P, W], I32, name="idx_i")
         idx_f = const.tile([P, W], F32, name="idx_f")
         w1_i = const.tile([P, P], I32, name="w1_i")
@@ -157,13 +162,28 @@ def tile_costvolume_kernel(tc, img1, img2, intri1, intri2, extri1, extri2, out_0
                 else:
                     nc.gpsimd.tensor_scalar(out=dst, in0=src, scalar1=1.0, scalar2=0.0, op0=ALU.mult, op1=ALU.add)
 
+        def pass_through(u):
+            pt = psp.tile([P, 2 * W], BF16, tag="pt", name="pt_%d" % u)
+            passed[u] = pt
+            for lo, hi in ((0, P), (P, PW)):
+                nc.tensor.matmul(
+                    out=pt[:, PACK * lo : PACK * hi],
+                    lhsT=ident_bf[:],
+                    rhs=raw[(1, u)][:, :, W - PW + lo : W - PW + hi].rearrange("p t w -> p w t"),
+                    start=True,
+                    stop=True,
+                )
+
         def regroup(u):
             grouped[u] = grpp.tile([P, 2, W, PACK], BF16, tag="grouped", name="grouped_%d" % u, align_bytes=64)
             cv = HEAD[u] if u < len(HEAD) else CV
             cg = 0 if u < len(HEAD) else CG
             regroup_part("g", u, 0, cg)
             regroup_part("v", u, cg, cg + cv)
-            regroup_part("s", u, cg + cv, 2 * W)
+            nc.scalar.copy(
+                out=grouped[u][:, 1, W - PW : W, :].rearrange("p w t -> p (w t)"), in_=passed[u][:, 0 : PACK * PW]
+            )
+            regroup_part("s", u, cg + cv, 2 * W - PW)
 
         def quantise(u):
             codes[u] = qp.tile([P, 2 * W], U32, tag="codes", name="codes_%d" % u, align_bytes=64)
@@ -354,6 +374,8 @@ def tile_costvolume_kernel(tc, img1, img2, intri1, intri2, extri1, extri2, out_0
             r = i + AHEAD
             if r + LOOKAHEAD < N_UNITS:
                 load(r + LOOKAHEAD)
+            if r < N_UNITS:
+                pass_through(r)
             if 0 <= i + 1 < N_UNITS:
                 quantise(i + 1)
                 multiply(i + 1)

@@ -29,9 +29,9 @@ SCALE = 1.0 / math.sqrt(C)
 BIG = 3.0e38
 FLOPS = 2 * B * H * W * W * C
 
-CV = 0
+CV = 208
 HEAD = [680, 512]
-CG = 288
+CG = 160
 PIN = True
 AHEAD = 4
 BATCH = 4
@@ -42,7 +42,7 @@ def tile_costvolume_kernel(tc, img1, img2, intri1, intri2, extri1, extri2, out_0
     nc = tc.nc
     with ExitStack() as ctx:
         const = ctx.enter_context(tc.tile_pool(name="const", bufs=1))
-        rawp = ctx.enter_context(tc.tile_pool(name="rawp", bufs=LOOKAHEAD + 1))
+        rawp = ctx.enter_context(tc.tile_pool(name="rawp", bufs=LOOKAHEAD + 2))
         grpp = ctx.enter_context(tc.tile_pool(name="grpp", bufs=3))
         qp = ctx.enter_context(tc.tile_pool(name="qp", bufs=3))
         ep = ctx.enter_context(tc.tile_pool(name="ep", bufs=3))
@@ -135,6 +135,7 @@ def tile_costvolume_kernel(tc, img1, img2, intri1, intri2, extri1, extri2, out_0
         nc.gpsimd.memset(half[:], 0.5)
 
         bm_all = const.tile([P, N_UNITS * NT * NK], F32, name="bm_all")
+        nc.gpsimd.memset(bm_all[:], -BIG)
         m_all = const.tile([P, N_UNITS * NT], F32, name="m_all")
         bias_all = const.tile([P, N_UNITS * NT], F32, name="bias_all")
         sums = const.tile([P, N_UNITS * NT], F32, name="sums")
@@ -174,11 +175,15 @@ def tile_costvolume_kernel(tc, img1, img2, intri1, intri2, extri1, extri2, out_0
                     stop=True,
                 )
 
-        def regroup(u):
+        def shares(u):
+            return (0, HEAD[u]) if u < len(HEAD) else (CG, CV)
+
+        def regroup_first(u):
             grouped[u] = grpp.tile([P, 2, W, PACK], BF16, tag="grouped", name="grouped_%d" % u, align_bytes=64)
-            cv = HEAD[u] if u < len(HEAD) else CV
-            cg = 0 if u < len(HEAD) else CG
-            regroup_part("g", u, 0, cg)
+            regroup_part("g", u, 0, shares(u)[0])
+
+        def regroup_rest(u):
+            cg, cv = shares(u)
             regroup_part("v", u, cg, cg + cv)
             nc.scalar.copy(
                 out=grouped[u][:, 1, W - PW : W, :].rearrange("p w t -> p (w t)"), in_=passed[u][:, 0 : PACK * PW]
@@ -194,8 +199,8 @@ def tile_costvolume_kernel(tc, img1, img2, intri1, intri2, extri1, extri2, out_0
                 in_=grouped[u][:].rearrange("p g w j -> p (g w j)"),
             )
 
-        def multiply(u):
-            for t in range(NT):
+        def multiply(u, tiles):
+            for t in tiles:
                 bank = psum.tile([P, W], F32, tag="bank", name="bank_%d_%d" % (u, t))
                 banks[(u, t)] = bank
                 nc.tensor.matmul_mx(
@@ -212,8 +217,8 @@ def tile_costvolume_kernel(tc, img1, img2, intri1, intri2, extri1, extri2, out_0
             for t in range(NT):
                 c0 = NT * NK * u + NK * t
                 nc.vector.tensor_reduce(
-                    out=bm_all[:, c0 : c0 + NK],
-                    in_=banks[(u, t)][:].rearrange("p (k r) -> p k r", r=QUAD),
+                    out=bm_all[:, c0 : c0 + NQD * (t + 1)],
+                    in_=banks[(u, t)][:, 0 : P * (t + 1)].rearrange("p (k r) -> p k r", r=QUAD),
                     axis=AX.X,
                     op=ALU.max,
                 )
@@ -374,11 +379,13 @@ def tile_costvolume_kernel(tc, img1, img2, intri1, intri2, extri1, extri2, out_0
             r = i + AHEAD
             if r + LOOKAHEAD < N_UNITS:
                 load(r + LOOKAHEAD)
-            if r < N_UNITS:
-                pass_through(r)
-            if 0 <= i + 1 < N_UNITS:
+            if 1 <= i + 1 < N_UNITS:
                 quantise(i + 1)
-                multiply(i + 1)
+                multiply(i + 1, range(NT - 1))
+            if 0 <= r - 1 < N_UNITS:
+                pass_through(r - 1)
+            if 1 <= i + 1 < N_UNITS:
+                multiply(i + 1, [NT - 1])
             if 0 <= i - 3 < N_UNITS and (i - 3) % BATCH == BATCH - 1:
                 diag_max((i - 3) // BATCH)
             if 0 <= i < N_UNITS:
@@ -409,7 +416,12 @@ def tile_costvolume_kernel(tc, img1, img2, intri1, intri2, extri1, extri2, out_0
                 row_max_all(i)
                 exponentials(i)
             if r < N_UNITS:
-                regroup(r)
+                regroup_first(r)
+            if 0 <= r - 1 < N_UNITS:
+                regroup_rest(r - 1)
+            if r - 1 == 1:
+                quantise(0)
+                multiply(0, range(NT))
             if 0 <= i - 1 < N_UNITS:
                 realign(i - 1)
             if 0 <= i - 2 < N_UNITS:

@@ -30,7 +30,7 @@ BIG = 3.0e38
 FLOPS = 2 * B * H * W * W * C
 
 CV = 208
-HEAD = [680, 512]
+HEAD = [[("s", 0, 160), ("v", 160, 832)], [("v", 0, 512), ("s", 512, 832)]]
 CG = 160
 PIN = True
 AHEAD = 4
@@ -106,13 +106,13 @@ def tile_costvolume_kernel(tc, img1, img2, intri1, intri2, extri1, extri2, out_0
             )
         ident = const.tile([P, P], F32, name="ident")
         make_identity(nc, ident[:])
-        bigt = const.tile([P, NT * NK], F32, name="bigt")
-        cap = const.tile([P, NT * NK], F32, name="cap")
+        bigt = const.tile([P, NQD], F32, name="bigt")
+        cap = const.tile([P, NQD], F32, name="cap")
         nc.vector.memset(bigt[:], BIG)
         nc.gpsimd.affine_select(
             out=cap[:],
             in_=bigt[:],
-            pattern=[[P, NT], [-QUAD, NK]],
+            pattern=[[-QUAD, NQD]],
             compare_op=ALU.is_ge,
             fill=-BIG,
             base=-QUAD,
@@ -134,7 +134,7 @@ def tile_costvolume_kernel(tc, img1, img2, intri1, intri2, extri1, extri2, out_0
         half = const.tile([P, B], F32, name="half")
         nc.gpsimd.memset(half[:], 0.5)
 
-        bm_all = const.tile([P, N_UNITS * NT * NK], F32, name="bm_all")
+        bm_all = const.tile([P, N_UNITS, NT * (NK + NQD)], F32, name="bm_all")
         nc.gpsimd.memset(bm_all[:], -BIG)
         m_all = const.tile([P, N_UNITS * NT], F32, name="m_all")
         bias_all = const.tile([P, N_UNITS * NT], F32, name="bias_all")
@@ -176,19 +176,23 @@ def tile_costvolume_kernel(tc, img1, img2, intri1, intri2, extri1, extri2, out_0
                 )
 
         def shares(u):
-            return (0, HEAD[u]) if u < len(HEAD) else (CG, CV)
+            if u < len(HEAD):
+                return HEAD[u]
+            return [("g", 0, CG), ("v", CG, CG + CV), ("s", CG + CV, 2 * W - PW)]
 
         def regroup_first(u):
             grouped[u] = grpp.tile([P, 2, W, PACK], BF16, tag="grouped", name="grouped_%d" % u, align_bytes=64)
-            regroup_part("g", u, 0, shares(u)[0])
+            for kind, lo, hi in shares(u):
+                if kind == "g":
+                    regroup_part(kind, u, lo, hi)
 
         def regroup_rest(u):
-            cg, cv = shares(u)
-            regroup_part("v", u, cg, cg + cv)
+            for kind, lo, hi in shares(u):
+                if kind != "g":
+                    regroup_part(kind, u, lo, hi)
             nc.scalar.copy(
                 out=grouped[u][:, 1, W - PW : W, :].rearrange("p w t -> p (w t)"), in_=passed[u][:, 0 : PACK * PW]
             )
-            regroup_part("s", u, cg + cv, 2 * W - PW)
 
         def quantise(u):
             codes[u] = qp.tile([P, 2 * W], U32, tag="codes", name="codes_%d" % u, align_bytes=64)
@@ -215,9 +219,8 @@ def tile_costvolume_kernel(tc, img1, img2, intri1, intri2, extri1, extri2, out_0
 
         def row_max(u):
             for t in range(NT):
-                c0 = NT * NK * u + NK * t
                 nc.vector.tensor_reduce(
-                    out=bm_all[:, c0 : c0 + NQD * (t + 1)],
+                    out=bm_all[:, u, NK * t : NK * t + NQD * (t + 1)],
                     in_=banks[(u, t)][:, 0 : P * (t + 1)].rearrange("p (k r) -> p k r", r=QUAD),
                     axis=AX.X,
                     op=ALU.max,
@@ -226,15 +229,15 @@ def tile_costvolume_kernel(tc, img1, img2, intri1, intri2, extri1, extri2, out_0
         def row_max_all(u):
             nc.vector.tensor_reduce(
                 out=m_all[:, NT * u : NT * (u + 1)],
-                in_=bm_all[:, NT * NK * u : NT * NK * (u + 1)].rearrange("p (t k) -> p t k", k=NK),
+                in_=bm_all[:, u, 0 : NT * NK].rearrange("p (t k) -> p t k", k=NK),
                 axis=AX.X,
                 op=ALU.max,
             )
 
-        def exponentials(u):
+        def exponentials(u, tiles):
             nc.scalar.mul(out=bias_all[:, NT * u : NT * (u + 1)], in_=m_all[:, NT * u : NT * (u + 1)], mul=-SCALE)
             etile[u] = ep.tile([P, NT * (W + P)], F32, tag="e", name="e_%d" % u)
-            for t in range(NT):
+            for t in tiles:
                 col = NT * u + t
                 nc.scalar.activation(
                     out=etile[u][:, W * t : W * (t + 1)],
@@ -275,10 +278,19 @@ def tile_costvolume_kernel(tc, img1, img2, intri1, intri2, extri1, extri2, out_0
                     accum_out=num_all[:, col : col + 1],
                 )
 
-        def diag_max(k):
+        def mask_diag_direct(u, qd):
+            rows = slice(QUAD * qd, QUAD * (qd + 1))
+            nc.vector.tensor_tensor(
+                out=dm_all[rows, u, :, :],
+                in0=etile[u][rows, :].rearrange("p (t s) -> p t s", s=W + P)[:, :, QUAD * qd : QUAD * (qd + 1)],
+                in1=tril[rows, :].unsqueeze(1).to_broadcast([QUAD, NT, QUAD]),
+                op=ALU.mult,
+            )
+
+        def diag_max(u0, u1):
             nc.vector.tensor_reduce(
-                out=dmax_all[:, NT * BATCH * k : NT * BATCH * (k + 1)],
-                in_=dm_all[:, BATCH * k : BATCH * (k + 1), :, :].rearrange("p u t r -> p (u t) r"),
+                out=dmax_all[:, NT * u0 : NT * u1],
+                in_=dm_all[:, u0:u1, :, :].rearrange("p u t r -> p (u t) r"),
                 axis=AX.X,
                 op=ALU.max,
             )
@@ -299,7 +311,9 @@ def tile_costvolume_kernel(tc, img1, img2, intri1, intri2, extri1, extri2, out_0
 
         def camera_b(base, fx):
             prod = const.tile([P, B], F32, name="kk")
-            nc.vector.tensor_tensor(out=prod[:], in0=base[:], in1=fx[:], op=ALU.mult)
+            nc.vector.scalar_tensor_tensor(
+                out=prod[:], in0=base[:], scalar=float(W), in1=fx[:], op0=ALU.mult, op1=ALU.mult
+            )
             return prod
 
         kk = None
@@ -307,15 +321,14 @@ def tile_costvolume_kernel(tc, img1, img2, intri1, intri2, extri1, extri2, out_0
         NC = N_UNITS * NT
         hc = NC // B
         hu = N_UNITS // B
-        pmm = const.tile([P, N_UNITS, NT * NK], F32, name="pmm")
         pm = const.tile([P, NC], F32, name="pm")
         arg = const.tile([P, NC], F32, name="arg")
         pe = const.tile([P, NC], F32, name="pe")
         rs = const.tile([P, NC], F32, name="rs")
-        cor = const.tile([P, NC], F32, name="cor")
+        t1 = const.tile([P, NC], F32, name="t1")
         df = const.tile([P, NC], F32, name="df")
         ab = const.tile([P, NC], F32, name="ab")
-        disp = const.tile([P, NC], F32, name="disp")
+        den = const.tile([P, NC], F32, name="den")
         rd = const.tile([P, NC], F32, name="rd")
         depth = const.tile([P, NC], F32, name="depth")
         cn = const.tile([P, NC], F32, name="cn")
@@ -324,49 +337,58 @@ def tile_costvolume_kernel(tc, img1, img2, intri1, intri2, extri1, extri2, out_0
         def cols(b):
             return slice(hc * b, hc * (b + 1))
 
-        def f_pmm(t):
-            n = NQD * (t + 1)
+        def f_cap(b):
+            view = bm_all[:].rearrange("p u (t s) -> p (u t) s", s=NK + NQD)[:, cols(b), 0:NQD]
             nc.vector.tensor_tensor(
-                out=pmm[:].rearrange("p u (t k) -> p u t k", k=NK)[:, :, t, 0:n],
-                in0=bm_all[:].rearrange("p (u t k) -> p u t k", t=NT, k=NK)[:, :, t, 0:n],
-                in1=cap[:, NK * t : NK * t + n].unsqueeze(1).to_broadcast([P, N_UNITS, n]),
-                op=ALU.min,
+                out=view, in0=view, in1=cap[:].unsqueeze(1).to_broadcast([P, hc, NQD]), op=ALU.min
             )
 
-        def f_pm(t):
-            n = NQD * (t + 1)
+        def f_pm(t, b):
             nc.vector.tensor_reduce(
-                out=pm[:].rearrange("p (u t) -> p u t", t=NT)[:, :, t],
-                in_=pmm[:].rearrange("p u (t k) -> p u t k", k=NK)[:, :, t, 0:n],
+                out=pm[:].rearrange("p (u t) -> p u t", t=NT)[:, hu * b : hu * (b + 1), t],
+                in_=bm_all[:, hu * b : hu * (b + 1), NK * t : NK * t + NQD * (t + 1)],
                 axis=AX.X,
                 op=ALU.max,
             )
 
+        def f_arg(b):
+            nc.vector.scalar_tensor_tensor(
+                out=arg[:, cols(b)], in0=pm[:, cols(b)], scalar=SCALE, in1=bias_all[:, cols(b)], op0=ALU.mult, op1=ALU.add
+            )
+
+        def f_pe(b):
+            nc.scalar.activation(out=pe[:, cols(b)], in_=arg[:, cols(b)], func=ACT.Exp)
+
         def f_rs(b):
             nc.vector.reciprocal(out=rs[:, cols(b)], in_=sums[:, cols(b)])
 
-        def f_cor(b):
-            nc.vector.tensor_tensor(out=cor[:, cols(b)], in0=num_all[:, cols(b)], in1=rs[:, cols(b)], op=ALU.mult)
+        def f_t1(b):
+            nc.vector.tensor_tensor(out=t1[:, cols(b)], in0=sums[:, cols(b)], in1=w1_f[:, cols(b)], op=ALU.mult)
 
         def f_df(b):
-            nc.vector.tensor_tensor(out=df[:, cols(b)], in0=cor[:, cols(b)], in1=w1_f[:, cols(b)], op=ALU.subtract)
+            nc.vector.tensor_tensor(out=df[:, cols(b)], in0=num_all[:, cols(b)], in1=t1[:, cols(b)], op=ALU.subtract)
 
         def f_ab(b):
             nc.vector.scalar_tensor_tensor(
                 out=ab[:, cols(b)], in0=df[:, cols(b)], scalar=-1.0, in1=df[:, cols(b)], op0=ALU.mult, op1=ALU.max
             )
 
-        def f_disp(b):
-            nc.vector.tensor_scalar(
-                out=disp[:, cols(b)], in0=ab[:, cols(b)], scalar1=1.0 / W, scalar2=0.1, op0=ALU.mult, op1=ALU.max
+        def f_den(b):
+            nc.vector.scalar_tensor_tensor(
+                out=den[:, cols(b)], in0=sums[:, cols(b)], scalar=0.1 * W, in1=ab[:, cols(b)], op0=ALU.mult, op1=ALU.max
             )
 
         def f_rd(b):
-            nc.vector.reciprocal(out=rd[:, cols(b)], in_=disp[:, cols(b)])
+            nc.vector.reciprocal(out=rd[:, cols(b)], in_=den[:, cols(b)])
 
         def f_depth(b):
-            nc.vector.tensor_scalar(
-                out=depth[:, cols(b)], in0=rd[:, cols(b)], scalar1=kk[:, b : b + 1], scalar2=None, op0=ALU.mult
+            nc.vector.scalar_tensor_tensor(
+                out=depth[:, cols(b)],
+                in0=rd[:, cols(b)],
+                scalar=kk[:, b : b + 1],
+                in1=sums[:, cols(b)],
+                op0=ALU.mult,
+                op1=ALU.mult,
             )
 
         def f_cn(b):
@@ -375,7 +397,27 @@ def tile_costvolume_kernel(tc, img1, img2, intri1, intri2, extri1, extri2, out_0
         def f_conf(b):
             nc.vector.tensor_tensor(out=conf[:, cols(b)], in0=cn[:, cols(b)], in1=rs[:, cols(b)], op=ALU.mult)
 
-        for i in range(-AHEAD, N_UNITS + 2):
+        early = [
+            lambda: f_cap(0),
+            lambda: f_t1(0),
+            lambda: f_pm(3, 0),
+            lambda: f_rs(0),
+            lambda: f_pm(2, 0),
+            lambda: f_df(0),
+            lambda: f_pm(1, 0),
+            lambda: f_ab(0),
+            lambda: f_pm(0, 0),
+            lambda: f_den(0),
+            lambda: f_arg(0),
+            lambda: f_rd(0),
+            lambda: f_pe(0),
+            lambda: f_depth(0),
+            lambda: f_cn(0),
+            lambda: f_conf(0),
+        ]
+        last = N_UNITS - 1
+
+        for i in range(-AHEAD, N_UNITS):
             r = i + AHEAD
             if r + LOOKAHEAD < N_UNITS:
                 load(r + LOOKAHEAD)
@@ -386,35 +428,15 @@ def tile_costvolume_kernel(tc, img1, img2, intri1, intri2, extri1, extri2, out_0
                 pass_through(r - 1)
             if 1 <= i + 1 < N_UNITS:
                 multiply(i + 1, [NT - 1])
-            if 0 <= i - 3 < N_UNITS and (i - 3) % BATCH == BATCH - 1:
-                diag_max((i - 3) // BATCH)
-            if 0 <= i < N_UNITS:
+            if i - 3 >= 0 and (i - 3) % BATCH == BATCH - 1:
+                diag_max(i - 2 - BATCH, i - 2)
+            if i >= 0:
                 row_max(i)
-            if i == N_UNITS:
-                f_pmm(3)
-                f_rs(0)
-                f_pmm(2)
-                f_cor(0)
-                f_pm(3)
-                f_df(0)
-                f_pmm(1)
-                f_ab(0)
-                f_pm(2)
-                f_disp(0)
-                f_pmm(0)
-                f_rd(0)
-                f_pm(1)
-                f_depth(0)
-                f_pm(0)
-                nc.vector.scalar_tensor_tensor(
-                    out=arg[:], in0=pm[:], scalar=SCALE, in1=bias_all[:], op0=ALU.mult, op1=ALU.add
-                )
-                nc.scalar.activation(out=pe[:], in_=arg[:], func=ACT.Exp)
-            if 0 <= i - 1 < N_UNITS:
-                weighted_sums(i - 1, [0] if i == N_UNITS else [NT - 1])
-            if 0 <= i < N_UNITS:
+            if i - 1 >= 0:
+                weighted_sums(i - 1, [0])
+            if i >= 0:
                 row_max_all(i)
-                exponentials(i)
+                exponentials(i, range(NT) if i < last else [3, 2, 1, 0])
             if r < N_UNITS:
                 regroup_first(r)
             if 0 <= r - 1 < N_UNITS:
@@ -422,37 +444,52 @@ def tile_costvolume_kernel(tc, img1, img2, intri1, intri2, extri1, extri2, out_0
             if r - 1 == 1:
                 quantise(0)
                 multiply(0, range(NT))
-            if 0 <= i - 1 < N_UNITS:
+            if i - 1 >= 0:
                 realign(i - 1)
-            if 0 <= i - 2 < N_UNITS:
+            if i - 2 >= 0:
                 mask_diag(i - 2)
-            if 0 <= i - 1 < N_UNITS:
-                weighted_sums(i - 1, [1, 2, 3] if i == N_UNITS else [0, 1, 2])
+            if i - 1 >= 0:
+                weighted_sums(i - 1, [1, 2, 3])
             if i == 4:
                 cam = camera_a()
             if i == 6:
                 kk = camera_b(cam[0], cam[1])
+            if i >= hu + 3:
+                for step in early[2 * (i - hu - 3) : 2 * (i - hu - 3) + 2]:
+                    step()
 
+        mask_diag(last - 1)
+        f_cap(1)
+        f_pm(3, 1)
+        f_pm(2, 1)
+        f_pm(1, 1)
+        f_pm(0, 1)
+        f_arg(1)
+        f_pe(1)
+        weighted_sums(last, [3, 2, 1, 0])
+        f_t1(1)
         f_rs(1)
-        f_cn(0)
-        f_cor(1)
-        f_conf(0)
+        diag_max(N_UNITS - BATCH, last)
         f_df(1)
-        diag_max(N_UNITS // BATCH - 1)
-        f_cn(1)
+        mask_diag_direct(last, 0)
         f_ab(1)
-        f_conf(1)
-        f_disp(1)
+        mask_diag_direct(last, 1)
+        f_den(1)
+        mask_diag_direct(last, 2)
         f_rd(1)
+        mask_diag_direct(last, 3)
         f_depth(1)
+        diag_max(last, N_UNITS)
+        f_cn(1)
+        f_conf(1)
 
         pt0 = psum.tile([P, W], F32, tag="bank", name="pt0")
         pt1 = psum.tile([P, W], F32, tag="bank", name="pt1")
         o0 = const.tile([P, P], F32, name="o0")
         o1 = const.tile([P, P], F32, name="o1")
-        nc.tensor.transpose(out=pt1[:, 0:P], in_=conf[:], identity=ident[:])
-        nc.scalar.copy(out=o1[:], in_=pt1[:, 0:P])
-        nc.scalar.dma_start(out=out_1.rearrange("b o h (t p) -> (b o h t) p", p=P), in_=o1[:])
         nc.tensor.transpose(out=pt0[:, 0:P], in_=depth[:], identity=ident[:])
         nc.scalar.copy(out=o0[:], in_=pt0[:, 0:P])
         nc.sync.dma_start(out=out_0.rearrange("b o h (t p) -> (b o h t) p", p=P), in_=o0[:])
+        nc.tensor.transpose(out=pt1[:, 0:P], in_=conf[:], identity=ident[:])
+        nc.scalar.copy(out=o1[:], in_=pt1[:, 0:P])
+        nc.scalar.dma_start(out=out_1.rearrange("b o h (t p) -> (b o h t) p", p=P), in_=o1[:])

@@ -31,7 +31,7 @@ FLOPS = 2 * B * H * W * W * C
 
 CV = 208
 HEAD = [[("s", 0, 160), ("v", 160, 832)], [("v", 0, 512), ("s", 512, 832)]]
-CG = 160
+CG = 128
 PIN = True
 AHEAD = 4
 BATCH = 4

@@ -29,7 +29,7 @@ SCALE = 1.0 / math.sqrt(C)
 BIG = 3.0e38
 FLOPS = 2 * B * H * W * W * C
 
-CV = 208
+CV = 168
 HEAD = [[("s", 0, 160), ("v", 160, 832)], [("v", 0, 512), ("s", 512, 832)]]
 CG = 128
 PIN = True

@@ -29,9 +29,9 @@ SCALE = 1.0 / math.sqrt(C)
 BIG = 3.0e38
 FLOPS = 2 * B * H * W * W * C
 
-CV = 168
+CV = 0
 HEAD = [[("s", 0, 160), ("v", 160, 832)], [("v", 0, 512), ("s", 512, 832)]]
-CG = 128
+CG = 368
 PIN = True
 AHEAD = 4
 BATCH = 4
@@ -46,8 +46,9 @@ def tile_costvolume_kernel(tc, img1, img2, intri1, intri2, extri1, extri2, out_0
         grpp = ctx.enter_context(tc.tile_pool(name="grpp", bufs=3))
         qp = ctx.enter_context(tc.tile_pool(name="qp", bufs=3))
         ep = ctx.enter_context(tc.tile_pool(name="ep", bufs=3))
-        psum = ctx.enter_context(tc.psum_pool(name="psum", bufs=7))
+        psum = ctx.enter_context(tc.psum_pool(name="psum", bufs=5))
         psp = ctx.enter_context(tc.psum_pool(name="psp", bufs=1))
+        pst = ctx.enter_context(tc.psum_pool(name="pst", bufs=1))
         if PIN:
             ctx.enter_context(tc.manual_schedule())
 
@@ -264,6 +265,21 @@ def tile_costvolume_kernel(tc, img1, img2, intri1, intri2, extri1, extri2, out_0
                 op=ALU.mult,
             )
 
+        tab_a = pst.tile([P, W], F32, tag="tab_a", name="tab_a")
+        tab_b = pst.tile([P, W], F32, tag="tab_b", name="tab_b")
+        weights = {
+            0: tab_b[:, 3 * P : 4 * P],
+            1: wtab[:, offs[1] : offs[1] + 2 * P],
+            2: tab_b[:, 0 : 3 * P],
+            3: tab_a[:, 0 : 4 * P],
+        }
+
+        def tables_to_psum():
+            for t in (3, 2, 0):
+                nc.tensor.matmul(
+                    out=weights[t], lhsT=ident[:], rhs=wtab[:, offs[t] : offs[t] + P * (t + 1)], start=True, stop=True
+                )
+
         def weighted_sums(u, tiles):
             for t in tiles:
                 n = P * (t + 1)
@@ -272,7 +288,7 @@ def tile_costvolume_kernel(tc, img1, img2, intri1, intri2, extri1, extri2, out_0
                     out=junk[u % 2][:, offs[t] : offs[t] + n],
                     in0=etile[u][:, W * t : W * t + n],
                     scalar=1.0,
-                    in1=wtab[:, offs[t] : offs[t] + n],
+                    in1=weights[t],
                     op0=ALU.mult,
                     op1=ALU.mult,
                     accum_out=num_all[:, col : col + 1],
@@ -423,11 +439,13 @@ def tile_costvolume_kernel(tc, img1, img2, intri1, intri2, extri1, extri2, out_0
                 load(r + LOOKAHEAD)
             if 1 <= i + 1 < N_UNITS:
                 quantise(i + 1)
-                multiply(i + 1, range(NT - 1))
+                multiply(i + 1, [0])
             if 0 <= r - 1 < N_UNITS:
                 pass_through(r - 1)
+            if i == 0:
+                tables_to_psum()
             if 1 <= i + 1 < N_UNITS:
-                multiply(i + 1, [NT - 1])
+                multiply(i + 1, [1, 2, 3])
             if i - 3 >= 0 and (i - 3) % BATCH == BATCH - 1:
                 diag_max(i - 2 - BATCH, i - 2)
             if i >= 0:
@@ -437,6 +455,8 @@ def tile_costvolume_kernel(tc, img1, img2, intri1, intri2, extri1, extri2, out_0
             if i >= 0:
                 row_max_all(i)
                 exponentials(i, range(NT) if i < last else [3, 2, 1, 0])
+            if i - 1 >= 0:
+                weighted_sums(i - 1, [3, 2])
             if r < N_UNITS:
                 regroup_first(r)
             if 0 <= r - 1 < N_UNITS:
@@ -449,7 +469,7 @@ def tile_costvolume_kernel(tc, img1, img2, intri1, intri2, extri1, extri2, out_0
             if i - 2 >= 0:
                 mask_diag(i - 2)
             if i - 1 >= 0:
-                weighted_sums(i - 1, [1, 2, 3])
+                weighted_sums(i - 1, [1])
             if i == 4:
                 cam = camera_a()
             if i == 6:

@@ -31,7 +31,7 @@ FLOPS = 2 * B * H * W * W * C
 
 CV = 0
 HEAD = [[("s", 0, 160), ("v", 160, 832)], [("v", 0, 512), ("s", 512, 832)]]
-CG = 368
+CG = 432
 PIN = True
 AHEAD = 4
 BATCH = 4
@@ -46,7 +46,7 @@ def tile_costvolume_kernel(tc, img1, img2, intri1, intri2, extri1, extri2, out_0
         grpp = ctx.enter_context(tc.tile_pool(name="grpp", bufs=3))
         qp = ctx.enter_context(tc.tile_pool(name="qp", bufs=3))
         ep = ctx.enter_context(tc.tile_pool(name="ep", bufs=3))
-        psum = ctx.enter_context(tc.psum_pool(name="psum", bufs=5))
+        psum = ctx.enter_context(tc.psum_pool(name="psum", bufs=4))
         psp = ctx.enter_context(tc.psum_pool(name="psp", bufs=1))
         pst = ctx.enter_context(tc.psum_pool(name="pst", bufs=1))
         if PIN:
@@ -267,15 +267,16 @@ def tile_costvolume_kernel(tc, img1, img2, intri1, intri2, extri1, extri2, out_0
 
         tab_a = pst.tile([P, W], F32, tag="tab_a", name="tab_a")
         tab_b = pst.tile([P, W], F32, tag="tab_b", name="tab_b")
+        tab_c = pst.tile([P, W], F32, tag="tab_c", name="tab_c")
         weights = {
             0: tab_b[:, 3 * P : 4 * P],
-            1: wtab[:, offs[1] : offs[1] + 2 * P],
+            1: tab_c[:, 0 : 2 * P],
             2: tab_b[:, 0 : 3 * P],
             3: tab_a[:, 0 : 4 * P],
         }
 
         def tables_to_psum():
-            for t in (3, 2, 0):
+            for t in (3, 2, 1, 0):
                 nc.tensor.matmul(
                     out=weights[t], lhsT=ident[:], rhs=wtab[:, offs[t] : offs[t] + P * (t + 1)], start=True, stop=True
                 )
@@ -439,13 +440,12 @@ def tile_costvolume_kernel(tc, img1, img2, intri1, intri2, extri1, extri2, out_0
                 load(r + LOOKAHEAD)
             if 1 <= i + 1 < N_UNITS:
                 quantise(i + 1)
-                multiply(i + 1, [0])
             if 0 <= r - 1 < N_UNITS:
                 pass_through(r - 1)
             if i == 0:
                 tables_to_psum()
             if 1 <= i + 1 < N_UNITS:
-                multiply(i + 1, [1, 2, 3])
+                multiply(i + 1, range(NT))
             if i - 3 >= 0 and (i - 3) % BATCH == BATCH - 1:
                 diag_max(i - 2 - BATCH, i - 2)
             if i >= 0:
@@ -456,7 +456,7 @@ def tile_costvolume_kernel(tc, img1, img2, intri1, intri2, extri1, extri2, out_0
                 row_max_all(i)
                 exponentials(i, range(NT) if i < last else [3, 2, 1, 0])
             if i - 1 >= 0:
-                weighted_sums(i - 1, [3, 2])
+                weighted_sums(i - 1, [3, 2, 1])
             if r < N_UNITS:
                 regroup_first(r)
             if 0 <= r - 1 < N_UNITS:
@@ -468,8 +468,6 @@ def tile_costvolume_kernel(tc, img1, img2, intri1, intri2, extri1, extri2, out_0
                 realign(i - 1)
             if i - 2 >= 0:
                 mask_diag(i - 2)
-            if i - 1 >= 0:
-                weighted_sums(i - 1, [1])
             if i == 4:
                 cam = camera_a()
             if i == 6:

@@ -31,7 +31,7 @@ FLOPS = 2 * B * H * W * W * C
 
 CV = 0
 HEAD = [[("s", 0, 160), ("v", 160, 832)], [("v", 0, 512), ("s", 512, 832)]]
-CG = 432
+CG = 408
 PIN = True
 AHEAD = 4
 BATCH = 4

@@ -25,6 +25,7 @@ QUAD = 32
 NK = W // QUAD
 NQD = P // QUAD
 LOOKAHEAD = 5
+ORDER = (3, 2, 1, 0)
 SCALE = 1.0 / math.sqrt(C)
 BIG = 3.0e38
 FLOPS = 2 * B * H * W * W * C
@@ -219,7 +220,7 @@ def tile_costvolume_kernel(tc, img1, img2, intri1, intri2, extri1, extri2, out_0
                 )
 
         def row_max(u):
-            for t in range(NT):
+            for t in ORDER:
                 nc.vector.tensor_reduce(
                     out=bm_all[:, u, NK * t : NK * t + NQD * (t + 1)],
                     in_=banks[(u, t)][:, 0 : P * (t + 1)].rearrange("p (k r) -> p k r", r=QUAD),
@@ -445,7 +446,7 @@ def tile_costvolume_kernel(tc, img1, img2, intri1, intri2, extri1, extri2, out_0
             if i == 0:
                 tables_to_psum()
             if 1 <= i + 1 < N_UNITS:
-                multiply(i + 1, range(NT))
+                multiply(i + 1, ORDER)
             if i - 3 >= 0 and (i - 3) % BATCH == BATCH - 1:
                 diag_max(i - 2 - BATCH, i - 2)
             if i >= 0:
@@ -454,7 +455,7 @@ def tile_costvolume_kernel(tc, img1, img2, intri1, intri2, extri1, extri2, out_0
                 weighted_sums(i - 1, [0])
             if i >= 0:
                 row_max_all(i)
-                exponentials(i, range(NT) if i < last else [3, 2, 1, 0])
+                exponentials(i, ORDER)
             if i - 1 >= 0:
                 weighted_sums(i - 1, [3, 2, 1])
             if r < N_UNITS:
@@ -463,7 +464,7 @@ def tile_costvolume_kernel(tc, img1, img2, intri1, intri2, extri1, extri2, out_0
                 regroup_rest(r - 1)
             if r - 1 == 1:
                 quantise(0)
-                multiply(0, range(NT))
+                multiply(0, ORDER)
             if i - 1 >= 0:
                 realign(i - 1)
             if i - 2 >= 0:

@@ -219,8 +219,8 @@ def tile_costvolume_kernel(tc, img1, img2, intri1, intri2, extri1, extri2, out_0
                     stop=True,
                 )
 
-        def row_max(u):
-            for t in ORDER:
+        def row_max(u, tiles):
+            for t in tiles:
                 nc.vector.tensor_reduce(
                     out=bm_all[:, u, NK * t : NK * t + NQD * (t + 1)],
                     in_=banks[(u, t)][:, 0 : P * (t + 1)].rearrange("p (k r) -> p k r", r=QUAD),
@@ -228,18 +228,21 @@ def tile_costvolume_kernel(tc, img1, img2, intri1, intri2, extri1, extri2, out_0
                     op=ALU.max,
                 )
 
-        def row_max_all(u):
+        def row_max_pair(u, pair):
+            lo = 2 * pair
             nc.vector.tensor_reduce(
-                out=m_all[:, NT * u : NT * (u + 1)],
-                in_=bm_all[:, u, 0 : NT * NK].rearrange("p (t k) -> p t k", k=NK),
+                out=m_all[:, NT * u + lo : NT * u + lo + 2],
+                in_=bm_all[:, u, NK * lo : NK * (lo + 2)].rearrange("p (t k) -> p t k", k=NK),
                 axis=AX.X,
                 op=ALU.max,
             )
 
-        def exponentials(u, tiles):
-            nc.scalar.mul(out=bias_all[:, NT * u : NT * (u + 1)], in_=m_all[:, NT * u : NT * (u + 1)], mul=-SCALE)
-            etile[u] = ep.tile([P, NT * (W + P)], F32, tag="e", name="e_%d" % u)
-            for t in tiles:
+        def exponentials(u, pair):
+            c0 = NT * u + 2 * pair
+            nc.scalar.mul(out=bias_all[:, c0 : c0 + 2], in_=m_all[:, c0 : c0 + 2], mul=-SCALE)
+            if pair == 1:
+                etile[u] = ep.tile([P, NT * (W + P)], F32, tag="e", name="e_%d" % u)
+            for t in (2 * pair + 1, 2 * pair):
                 col = NT * u + t
                 nc.scalar.activation(
                     out=etile[u][:, W * t : W * (t + 1)],
@@ -450,14 +453,20 @@ def tile_costvolume_kernel(tc, img1, img2, intri1, intri2, extri1, extri2, out_0
             if i - 3 >= 0 and (i - 3) % BATCH == BATCH - 1:
                 diag_max(i - 2 - BATCH, i - 2)
             if i >= 0:
-                row_max(i)
+                row_max(i, [3, 2])
             if i - 1 >= 0:
                 weighted_sums(i - 1, [0])
             if i >= 0:
-                row_max_all(i)
-                exponentials(i, ORDER)
+                row_max_pair(i, 1)
+                exponentials(i, 1)
+                row_max(i, [1, 0])
             if i - 1 >= 0:
-                weighted_sums(i - 1, [3, 2, 1])
+                weighted_sums(i - 1, [1])
+            if i >= 0:
+                row_max_pair(i, 0)
+                exponentials(i, 0)
+            if i - 1 >= 0:
+                weighted_sums(i - 1, [2, 3])
             if r < N_UNITS:
                 regroup_first(r)
             if 0 <= r - 1 < N_UNITS:

@@ -192,6 +192,9 @@ def tile_costvolume_kernel(tc, img1, img2, intri1, intri2, extri1, extri2, out_0
             for kind, lo, hi in shares(u):
                 if kind != "g":
                     regroup_part(kind, u, lo, hi)
+            copy_passed(u)
+
+        def copy_passed(u):
             nc.scalar.copy(
                 out=grouped[u][:, 1, W - PW : W, :].rearrange("p w t -> p (w t)"), in_=passed[u][:, 0 : PACK * PW]
             )
@@ -237,9 +240,11 @@ def tile_costvolume_kernel(tc, img1, img2, intri1, intri2, extri1, extri2, out_0
                 op=ALU.max,
             )
 
-        def exponentials(u, pair):
+        def biases(u, pair):
             c0 = NT * u + 2 * pair
             nc.scalar.mul(out=bias_all[:, c0 : c0 + 2], in_=m_all[:, c0 : c0 + 2], mul=-SCALE)
+
+        def exponentials(u, pair):
             if pair == 1:
                 etile[u] = ep.tile([P, NT * (W + P)], F32, tag="e", name="e_%d" % u)
             for t in (2 * pair + 1, 2 * pair):
@@ -458,18 +463,26 @@ def tile_costvolume_kernel(tc, img1, img2, intri1, intri2, extri1, extri2, out_0
                 weighted_sums(i - 1, [0])
             if i >= 0:
                 row_max_pair(i, 1)
+                biases(i, 1)
+                if r - 1 < N_UNITS:
+                    regroup_part("s", r - 1, CG + CV, W)
                 exponentials(i, 1)
                 row_max(i, [1, 0])
             if i - 1 >= 0:
                 weighted_sums(i - 1, [1])
             if i >= 0:
                 row_max_pair(i, 0)
+                biases(i, 0)
+                if r - 1 < N_UNITS:
+                    copy_passed(r - 1)
                 exponentials(i, 0)
+                if r - 1 < N_UNITS:
+                    regroup_part("s", r - 1, W, 2 * W - PW)
             if i - 1 >= 0:
                 weighted_sums(i - 1, [2, 3])
             if r < N_UNITS:
                 regroup_first(r)
-            if 0 <= r - 1 < N_UNITS:
+            if i < 0 <= r - 1:
                 regroup_rest(r - 1)
             if r - 1 == 1:
                 quantise(0)

@@ -8,7 +8,6 @@ from concourse.masks import make_identity
 
 F32 = mybir.dt.float32
 BF16 = mybir.dt.bfloat16
-I32 = mybir.dt.int32
 U32 = mybir.dt.uint32
 U8 = mybir.dt.uint8
 FP8X4 = mybir.dt.float8_e4m3fn_x4
@@ -28,10 +27,11 @@ LOOKAHEAD = 5
 ORDER = (3, 2, 1, 0)
 SCALE = 1.0 / math.sqrt(C)
 BIG = 3.0e38
+SUM_CAP = 1.0e30
 FLOPS = 2 * B * H * W * W * C
 
 CV = 0
-HEAD = [[("s", 0, 160), ("v", 160, 832)], [("v", 0, 512), ("s", 512, 832)]]
+HEAD = [[("s", 0, 160), ("v", 160, 832), ("s", 832, 1024)], [("v", 0, 512), ("s", 512, 832)], [("g", 0, 408), ("s", 408, 512)]]
 CG = 408
 PIN = True
 AHEAD = 4
@@ -74,9 +74,10 @@ def tile_costvolume_kernel(tc, img1, img2, intri1, intri2, extri1, extri2, out_0
         in1 = const.tile([P, 18], BF16, name="in1")
         ex1 = const.tile([P, 32], BF16, name="ex1")
         ex2 = const.tile([P, 32], BF16, name="ex2")
-        nc.scalar.dma_start(out=in1[:], in_=intri1.rearrange("b r c -> (b r c)").partition_broadcast(P))
-        nc.scalar.dma_start(out=ex1[:], in_=extri1.rearrange("b r c -> (b r c)").partition_broadcast(P))
-        nc.scalar.dma_start(out=ex2[:], in_=extri2.rearrange("b r c -> (b r c)").partition_broadcast(P))
+
+        def load_cameras():
+            for dst, src in ((in1, intri1), (ex1, extri1), (ex2, extri2)):
+                nc.sync.dma_start(out=dst[:], in_=src.rearrange("b r c -> (b r c)").partition_broadcast(P))
 
         warm = const.tile([P, 1], F32, name="warm")
         warm2 = const.tile([P, 1], F32, name="warm2")
@@ -85,59 +86,64 @@ def tile_costvolume_kernel(tc, img1, img2, intri1, intri2, extri1, extri2, out_0
 
         ident_bf = const.tile([P, P], BF16, name="ident_bf")
         make_identity(nc, ident_bf[:])
-        idx_i = const.tile([P, W], I32, name="idx_i")
-        idx_f = const.tile([P, W], F32, name="idx_f")
-        w1_i = const.tile([P, P], I32, name="w1_i")
-        w1_f = const.tile([P, P], F32, name="w1_f")
-        nc.gpsimd.iota(idx_i[:], pattern=[[1, W]], base=0, channel_multiplier=0)
-        nc.gpsimd.iota(w1_i[:], pattern=[[0, N_UNITS], [P, NT]], base=0, channel_multiplier=1)
-        nc.vector.tensor_copy(out=idx_f[:], in_=idx_i[:])
-        nc.vector.tensor_copy(out=w1_f[:], in_=w1_i[:])
-        offs = [P * t * (t + 1) // 2 for t in range(NT)]
-        wtab = const.tile([P, P * NT * (NT + 1) // 2], F32, name="wtab")
-        for t in range(NT):
-            n = P * (t + 1)
-            nc.gpsimd.affine_select(
-                out=wtab[:, offs[t] : offs[t] + n],
-                in_=idx_f[:, 0:n],
-                pattern=[[-1, n]],
-                compare_op=ALU.is_ge,
-                fill=0.0,
-                base=P * t,
-                channel_multiplier=1,
-            )
         ident = const.tile([P, P], F32, name="ident")
         make_identity(nc, ident[:])
+        column_w = const.tile([P, NT, P], F32, name="column_w")
+        diag_w = const.tile([P, NT, P], F32, name="diag_w")
+        nc.gpsimd.iota(
+            column_w[:], pattern=[[P, NT], [0, P]], base=0, channel_multiplier=1, allow_small_or_imprecise_dtypes=True
+        )
+        nc.gpsimd.affine_select(
+            out=diag_w[:],
+            in_=column_w[:],
+            pattern=[[0, NT], [1, P]],
+            compare_op=ALU.is_ge,
+            fill=0.0,
+            base=0,
+            channel_multiplier=-1,
+        )
         bigt = const.tile([P, NQD], F32, name="bigt")
         cap = const.tile([P, NQD], F32, name="cap")
         nc.vector.memset(bigt[:], BIG)
-        nc.gpsimd.affine_select(
-            out=cap[:],
-            in_=bigt[:],
-            pattern=[[-QUAD, NQD]],
-            compare_op=ALU.is_ge,
-            fill=-BIG,
-            base=-QUAD,
-            channel_multiplier=1,
-        )
         ones = const.tile([P, QUAD], F32, name="ones")
         tril = const.tile([P, QUAD], F32, name="tril")
         nc.vector.memset(ones[:], 1.0)
-        for qd in range(NQD):
+        half = const.tile([P, B], F32, name="half")
+        w1_f = const.tile([P, P], F32, name="w1_f")
+
+        def late_tables():
+            for qd in range(NQD):
+                nc.gpsimd.affine_select(
+                    out=tril[QUAD * qd : QUAD * (qd + 1), :],
+                    in_=ones[QUAD * qd : QUAD * (qd + 1), :],
+                    pattern=[[-1, QUAD]],
+                    compare_op=ALU.is_ge,
+                    fill=0.0,
+                    base=0,
+                    channel_multiplier=1,
+                )
             nc.gpsimd.affine_select(
-                out=tril[QUAD * qd : QUAD * (qd + 1), :],
-                in_=ones[QUAD * qd : QUAD * (qd + 1), :],
-                pattern=[[-1, QUAD]],
+                out=cap[:],
+                in_=bigt[:],
+                pattern=[[-QUAD, NQD]],
                 compare_op=ALU.is_ge,
-                fill=0.0,
-                base=0,
+                fill=-BIG,
+                base=-QUAD,
                 channel_multiplier=1,
             )
-        half = const.tile([P, B], F32, name="half")
-        nc.gpsimd.memset(half[:], 0.5)
+            nc.gpsimd.memset(half[:], 0.5)
+            nc.gpsimd.iota(
+                w1_f[:],
+                pattern=[[0, N_UNITS], [P, NT]],
+                base=0,
+                channel_multiplier=1,
+                allow_small_or_imprecise_dtypes=True,
+            )
 
         bm_all = const.tile([P, N_UNITS, NT * (NK + NQD)], F32, name="bm_all")
-        nc.gpsimd.memset(bm_all[:], -BIG)
+        for t in range(NT - 1):
+            unused = bm_all[:, :, 0 : NT * NK].rearrange("p u (t k) -> p u t k", k=NK)[:, :, t, NQD * (t + 1) : NK]
+            nc.vector.memset(unused, -BIG)
         m_all = const.tile([P, N_UNITS * NT], F32, name="m_all")
         bias_all = const.tile([P, N_UNITS * NT], F32, name="bias_all")
         sums = const.tile([P, N_UNITS * NT], F32, name="sums")
@@ -145,6 +151,7 @@ def tile_costvolume_kernel(tc, img1, img2, intri1, intri2, extri1, extri2, out_0
         dmax_all = const.tile([P, N_UNITS * NT], F32, name="dmax_all")
         draw_all = const.tile([P, N_UNITS, NT, QUAD], F32, name="draw_all")
         dm_all = const.tile([P, N_UNITS, NT, QUAD], F32, name="dm_all")
+        offs = [P * t * (t + 1) // 2 for t in range(NT)]
         junk = [const.tile([P, P * NT * (NT + 1) // 2], F32, name="junk%d" % k) for k in range(2)]
 
         def regroup_part(kind, u, lo, hi):
@@ -192,7 +199,8 @@ def tile_costvolume_kernel(tc, img1, img2, intri1, intri2, extri1, extri2, out_0
             for kind, lo, hi in shares(u):
                 if kind != "g":
                     regroup_part(kind, u, lo, hi)
-            copy_passed(u)
+            if u == 1:
+                copy_passed(u)
 
         def copy_passed(u):
             nc.scalar.copy(
@@ -285,10 +293,10 @@ def tile_costvolume_kernel(tc, img1, img2, intri1, intri2, extri1, extri2, out_0
         }
 
         def tables_to_psum():
-            for t in (3, 2, 1, 0):
-                nc.tensor.matmul(
-                    out=weights[t], lhsT=ident[:], rhs=wtab[:, offs[t] : offs[t] + P * (t + 1)], start=True, stop=True
-                )
+            for t in range(NT):
+                for c in range(t + 1):
+                    src = diag_w if c == t else column_w
+                    nc.tensor.transpose(out=weights[t][:, P * c : P * (c + 1)], in_=src[:, c, :], identity=ident[:])
 
         def weighted_sums(u, tiles):
             for t in tiles:
@@ -321,35 +329,36 @@ def tile_costvolume_kernel(tc, img1, img2, intri1, intri2, extri1, extri2, out_0
                 op=ALU.max,
             )
 
-        def camera_a():
-            dd = const.tile([P, 32], F32, name="dd")
-            nc.vector.tensor_tensor(out=dd[:], in0=ex1[:], in1=ex2[:], op=ALU.subtract)
-            dv = dd[:].rearrange("p (b r c) -> p b r c", b=B, r=4)[:, :, 0:3, 3]
-            sq = const.tile([P, B, 3], F32, name="sq")
-            nc.vector.tensor_tensor(out=sq[:], in0=dv, in1=dv, op=ALU.mult)
-            ss = const.tile([P, B], F32, name="ss")
-            nc.vector.tensor_reduce(out=ss[:], in_=sq[:], axis=AX.X, op=ALU.add)
-            base = const.tile([P, B], F32, name="base")
-            nc.gpsimd.tensor_tensor(out=base[:], in0=ss[:], in1=half[:], op=ALU.pow)
-            fx = const.tile([P, B], F32, name="fx")
-            nc.vector.tensor_copy(out=fx[:], in_=in1[:].rearrange("p (b k) -> p b k", b=B)[:, :, 0])
-            return base, fx
+        dd = const.tile([P, 32], F32, name="dd")
+        sq = const.tile([P, B, 3], F32, name="sq")
+        ss = const.tile([P, B], F32, name="ss")
+        base = const.tile([P, B], F32, name="base")
+        fx = const.tile([P, B], F32, name="fx")
+        kk = const.tile([P, B], F32, name="kk")
 
-        def camera_b(base, fx):
-            prod = const.tile([P, B], F32, name="kk")
-            nc.vector.scalar_tensor_tensor(
-                out=prod[:], in0=base[:], scalar=float(W), in1=fx[:], op0=ALU.mult, op1=ALU.mult
-            )
-            return prod
+        def camera(step):
+            if step == 0:
+                nc.vector.tensor_tensor(out=dd[:], in0=ex1[:], in1=ex2[:], op=ALU.subtract)
+                nc.vector.tensor_copy(out=fx[:], in_=in1[:].rearrange("p (b k) -> p b k", b=B)[:, :, 0])
+            elif step == 1:
+                dv = dd[:].rearrange("p (b r c) -> p b r c", b=B, r=4)[:, :, 0:3, 3]
+                nc.vector.tensor_tensor(out=sq[:], in0=dv, in1=dv, op=ALU.mult)
+            elif step == 2:
+                nc.vector.tensor_reduce(out=ss[:], in_=sq[:], axis=AX.X, op=ALU.add)
+            elif step == 3:
+                nc.gpsimd.tensor_tensor(out=base[:], in0=ss[:], in1=half[:], op=ALU.pow)
+            elif step == 4:
+                nc.vector.scalar_tensor_tensor(
+                    out=kk[:], in0=base[:], scalar=float(W), in1=fx[:], op0=ALU.mult, op1=ALU.mult
+                )
 
-        kk = None
-        cam = None
         NC = N_UNITS * NT
         hc = NC // B
         hu = N_UNITS // B
         pm = const.tile([P, NC], F32, name="pm")
         arg = const.tile([P, NC], F32, name="arg")
         pe = const.tile([P, NC], F32, name="pe")
+        sc = const.tile([P, NC], F32, name="sc")
         rs = const.tile([P, NC], F32, name="rs")
         t1 = const.tile([P, NC], F32, name="t1")
         df = const.tile([P, NC], F32, name="df")
@@ -385,11 +394,23 @@ def tile_costvolume_kernel(tc, img1, img2, intri1, intri2, extri1, extri2, out_0
         def f_pe(b):
             nc.scalar.activation(out=pe[:, cols(b)], in_=arg[:, cols(b)], func=ACT.Exp)
 
+        def f_sc(b):
+            nc.vector.tensor_scalar(
+                out=sc[:, cols(b)], in0=sums[:, cols(b)], scalar1=SUM_CAP, scalar2=None, op0=ALU.min
+            )
+
         def f_rs(b):
-            nc.vector.reciprocal(out=rs[:, cols(b)], in_=sums[:, cols(b)])
+            nc.vector.reciprocal(out=rs[:, cols(b)], in_=sc[:, cols(b)])
 
         def f_t1(b):
-            nc.vector.tensor_tensor(out=t1[:, cols(b)], in0=sums[:, cols(b)], in1=w1_f[:, cols(b)], op=ALU.mult)
+            nc.vector.scalar_tensor_tensor(
+                out=t1[:, cols(b)],
+                in0=sums[:, cols(b)],
+                scalar=SUM_CAP,
+                in1=w1_f[:, cols(b)],
+                op0=ALU.min,
+                op1=ALU.mult,
+            )
 
         def f_df(b):
             nc.vector.tensor_tensor(out=df[:, cols(b)], in0=num_all[:, cols(b)], in1=t1[:, cols(b)], op=ALU.subtract)
@@ -401,7 +422,7 @@ def tile_costvolume_kernel(tc, img1, img2, intri1, intri2, extri1, extri2, out_0
 
         def f_den(b):
             nc.vector.scalar_tensor_tensor(
-                out=den[:, cols(b)], in0=sums[:, cols(b)], scalar=0.1 * W, in1=ab[:, cols(b)], op0=ALU.mult, op1=ALU.max
+                out=den[:, cols(b)], in0=sc[:, cols(b)], scalar=0.1 * W, in1=ab[:, cols(b)], op0=ALU.mult, op1=ALU.max
             )
 
         def f_rd(b):
@@ -412,7 +433,7 @@ def tile_costvolume_kernel(tc, img1, img2, intri1, intri2, extri1, extri2, out_0
                 out=depth[:, cols(b)],
                 in0=rd[:, cols(b)],
                 scalar=kk[:, b : b + 1],
-                in1=sums[:, cols(b)],
+                in1=sc[:, cols(b)],
                 op0=ALU.mult,
                 op1=ALU.mult,
             )
@@ -426,6 +447,7 @@ def tile_costvolume_kernel(tc, img1, img2, intri1, intri2, extri1, extri2, out_0
         early = [
             lambda: f_cap(0),
             lambda: f_t1(0),
+            lambda: f_sc(0),
             lambda: f_pm(3, 0),
             lambda: f_rs(0),
             lambda: f_pm(2, 0),
@@ -447,54 +469,66 @@ def tile_costvolume_kernel(tc, img1, img2, intri1, intri2, extri1, extri2, out_0
             r = i + AHEAD
             if r + LOOKAHEAD < N_UNITS:
                 load(r + LOOKAHEAD)
-            if 1 <= i + 1 < N_UNITS:
+            if 2 <= i + 1 < N_UNITS:
                 quantise(i + 1)
-            if 0 <= r - 1 < N_UNITS:
+            if 1 <= r - 1 < N_UNITS and i != 0:
                 pass_through(r - 1)
-            if i == 0:
+            if r - 1 == 0:
                 tables_to_psum()
-            if 1 <= i + 1 < N_UNITS:
+            if 2 <= i + 1 < N_UNITS:
                 multiply(i + 1, ORDER)
+            if r - 1 == 1:
+                quantise(0)
+                multiply(0, ORDER)
             if i - 3 >= 0 and (i - 3) % BATCH == BATCH - 1:
                 diag_max(i - 2 - BATCH, i - 2)
             if i >= 0:
                 row_max(i, [3, 2])
             if i - 1 >= 0:
-                weighted_sums(i - 1, [0])
+                weighted_sums(i - 1, [1])
             if i >= 0:
                 row_max_pair(i, 1)
                 biases(i, 1)
-                if r - 1 < N_UNITS:
+                if i == 0:
+                    copy_passed(2)
+                    pass_through(3)
+                elif r - 1 < N_UNITS:
                     regroup_part("s", r - 1, CG + CV, W)
                 exponentials(i, 1)
                 row_max(i, [1, 0])
             if i - 1 >= 0:
-                weighted_sums(i - 1, [1])
+                weighted_sums(i - 1, [2])
             if i >= 0:
                 row_max_pair(i, 0)
                 biases(i, 0)
-                if r - 1 < N_UNITS:
+                if i == 0:
+                    quantise(1)
+                    multiply(1, ORDER)
+                    regroup_part("v", 2, W, 2 * W - PW)
+                    regroup_part("s", r - 1, CG + CV, W)
+                elif r - 1 < N_UNITS:
                     copy_passed(r - 1)
                 exponentials(i, 0)
+                if i == 0:
+                    copy_passed(r - 1)
                 if r - 1 < N_UNITS:
                     regroup_part("s", r - 1, W, 2 * W - PW)
             if i - 1 >= 0:
-                weighted_sums(i - 1, [2, 3])
+                weighted_sums(i - 1, [3, 0])
+            if i == -1:
+                late_tables()
             if r < N_UNITS:
                 regroup_first(r)
             if i < 0 <= r - 1:
                 regroup_rest(r - 1)
-            if r - 1 == 1:
-                quantise(0)
-                multiply(0, ORDER)
             if i - 1 >= 0:
                 realign(i - 1)
             if i - 2 >= 0:
                 mask_diag(i - 2)
-            if i == 4:
-                cam = camera_a()
-            if i == 6:
-                kk = camera_b(cam[0], cam[1])
+            if i == 2:
+                load_cameras()
+            if 8 <= i < 13:
+                camera(i - 8)
             if i >= hu + 3:
                 for step in early[2 * (i - hu - 3) : 2 * (i - hu - 3) + 2]:
                     step()
@@ -509,9 +543,10 @@ def tile_costvolume_kernel(tc, img1, img2, intri1, intri2, extri1, extri2, out_0
         f_pe(1)
         weighted_sums(last, [3, 2, 1, 0])
         f_t1(1)
-        f_rs(1)
+        f_sc(1)
         diag_max(N_UNITS - BATCH, last)
         f_df(1)
+        f_rs(1)
         mask_diag_direct(last, 0)
         f_ab(1)
         mask_diag_direct(last, 1)

@@ -314,7 +314,7 @@ def tile_costvolume_kernel(tc, img1, img2, intri1, intri2, extri1, extri2, out_0
 
         def mask_diag_direct(u, qd):
             rows = slice(QUAD * qd, QUAD * (qd + 1))
-            nc.vector.tensor_tensor(
+            nc.gpsimd.tensor_tensor(
                 out=dm_all[rows, u, :, :],
                 in0=etile[u][rows, :].rearrange("p (t s) -> p t s", s=W + P)[:, :, QUAD * qd : QUAD * (qd + 1)],
                 in1=tril[rows, :].unsqueeze(1).to_broadcast([QUAD, NT, QUAD]),
@@ -444,25 +444,40 @@ def tile_costvolume_kernel(tc, img1, img2, intri1, intri2, extri1, extri2, out_0
         def f_conf(b):
             nc.vector.tensor_tensor(out=conf[:, cols(b)], in0=cn[:, cols(b)], in1=rs[:, cols(b)], op=ALU.mult)
 
-        early = [
-            lambda: f_cap(0),
-            lambda: f_t1(0),
-            lambda: f_sc(0),
-            lambda: f_pm(3, 0),
-            lambda: f_rs(0),
-            lambda: f_pm(2, 0),
-            lambda: f_df(0),
-            lambda: f_pm(1, 0),
-            lambda: f_ab(0),
-            lambda: f_pm(0, 0),
-            lambda: f_den(0),
-            lambda: f_arg(0),
-            lambda: f_rd(0),
-            lambda: f_pe(0),
-            lambda: f_depth(0),
-            lambda: f_cn(0),
-            lambda: f_conf(0),
-        ]
+        dq = const.tile([P, hc], F32, name="dq")
+
+        def g_t1():
+            nc.gpsimd.tensor_tensor(out=t1[:, cols(0)], in0=sc[:, cols(0)], in1=w1_f[:, cols(0)], op=ALU.mult)
+
+        def g_df():
+            nc.gpsimd.tensor_tensor(out=df[:, cols(0)], in0=num_all[:, cols(0)], in1=t1[:, cols(0)], op=ALU.subtract)
+
+        def s_ab():
+            nc.scalar.activation(out=ab[:, cols(0)], in_=df[:, cols(0)], func=ACT.Abs)
+
+        def g_depth():
+            nc.gpsimd.tensor_tensor(out=dq[:], in0=rd[:, cols(0)], in1=sc[:, cols(0)], op=ALU.mult)
+            nc.gpsimd.tensor_scalar(
+                out=depth[:, cols(0)], in0=dq[:], scalar1=kk[:, 0:1], scalar2=0.0, op0=ALU.mult, op1=ALU.add
+            )
+
+        def g_conf():
+            nc.gpsimd.tensor_tensor(out=conf[:, cols(0)], in0=cn[:, cols(0)], in1=rs[:, cols(0)], op=ALU.mult)
+
+        early = {
+            19: [lambda: f_cap(0)],
+            20: [lambda: f_sc(0), lambda: f_pm(3, 0)],
+            21: [lambda: f_rs(0), lambda: f_pm(2, 0)],
+            22: [lambda: f_pm(1, 0)],
+            23: [lambda: f_pm(0, 0)],
+            24: [lambda: f_arg(0)],
+            25: [lambda: f_pe(0)],
+            26: [lambda: f_cn(0)],
+            28: [g_t1, g_df, g_conf],
+            29: [s_ab],
+            30: [lambda: f_den(0)],
+            31: [lambda: f_rd(0), g_depth],
+        }
         last = N_UNITS - 1
 
         for i in range(-AHEAD, N_UNITS):
@@ -529,33 +544,31 @@ def tile_costvolume_kernel(tc, img1, img2, intri1, intri2, extri1, extri2, out_0
                 load_cameras()
             if 8 <= i < 13:
                 camera(i - 8)
-            if i >= hu + 3:
-                for step in early[2 * (i - hu - 3) : 2 * (i - hu - 3) + 2]:
-                    step()
+            for step in early.get(i, []):
+                step()
 
         mask_diag(last - 1)
+        for qd in range(NQD):
+            mask_diag_direct(last, qd)
+        weighted_sums(last, [3, 2])
+        f_t1(1)
+        weighted_sums(last, [1])
+        f_sc(1)
+        weighted_sums(last, [0])
         f_cap(1)
+        f_df(1)
         f_pm(3, 1)
+        f_ab(1)
         f_pm(2, 1)
+        f_den(1)
         f_pm(1, 1)
         f_pm(0, 1)
+        f_rd(1)
+        f_rs(1)
         f_arg(1)
         f_pe(1)
-        weighted_sums(last, [3, 2, 1, 0])
-        f_t1(1)
-        f_sc(1)
-        diag_max(N_UNITS - BATCH, last)
-        f_df(1)
-        f_rs(1)
-        mask_diag_direct(last, 0)
-        f_ab(1)
-        mask_diag_direct(last, 1)
-        f_den(1)
-        mask_diag_direct(last, 2)
-        f_rd(1)
-        mask_diag_direct(last, 3)
         f_depth(1)
-        diag_max(last, N_UNITS)
+        diag_max(N_UNITS - BATCH, N_UNITS)
         f_cn(1)
         f_conf(1)
 

@@ -31,7 +31,7 @@ SUM_CAP = 1.0e30
 FLOPS = 2 * B * H * W * W * C
 
 CV = 0
-HEAD = [[("s", 0, 160), ("v", 160, 832), ("s", 832, 1024)], [("v", 0, 512), ("s", 512, 832)], [("g", 0, 408), ("s", 408, 512)]]
+HEAD = [[("s", 0, 160), ("v", 160, 896), ("s", 896, 1024)], [("v", 0, 512), ("s", 512, 832)], [("g", 0, 408), ("s", 408, 512)]]
 CG = 408
 PIN = True
 AHEAD = 4
@@ -312,6 +312,21 @@ def tile_costvolume_kernel(tc, img1, img2, intri1, intri2, extri1, extri2, out_0
                     accum_out=num_all[:, col : col + 1],
                 )
 
+        weights_sb = const.tile([P, P], F32, name="weights_sb")
+        prod = [const.tile([P, P], F32, name="prod%d" % k) for k in range(2)]
+        summed = const.tile([P, P], F32, name="summed")
+
+        def tables_to_sbuf():
+            nc.scalar.copy(out=weights_sb[:], in_=weights[0])
+
+        def products(u):
+            nc.gpsimd.tensor_tensor(out=prod[u % 2][:], in0=etile[u][:, 0:P], in1=weights_sb[:], op=ALU.mult)
+
+        def add_up(u):
+            nc.scalar.activation(
+                out=summed[:], in_=prod[u % 2][:], func=ACT.Copy, accum_out=num_all[:, NT * u : NT * u + 1]
+            )
+
         def mask_diag_direct(u, qd):
             rows = slice(QUAD * qd, QUAD * (qd + 1))
             nc.gpsimd.tensor_tensor(
@@ -333,24 +348,24 @@ def tile_costvolume_kernel(tc, img1, img2, intri1, intri2, extri1, extri2, out_0
         sq = const.tile([P, B, 3], F32, name="sq")
         ss = const.tile([P, B], F32, name="ss")
         base = const.tile([P, B], F32, name="base")
-        fx = const.tile([P, B], F32, name="fx")
+        wb = const.tile([P, B], F32, name="wb")
         kk = const.tile([P, B], F32, name="kk")
 
-        def camera(step):
-            if step == 0:
-                nc.vector.tensor_tensor(out=dd[:], in0=ex1[:], in1=ex2[:], op=ALU.subtract)
-                nc.vector.tensor_copy(out=fx[:], in_=in1[:].rearrange("p (b k) -> p b k", b=B)[:, :, 0])
-            elif step == 1:
-                dv = dd[:].rearrange("p (b r c) -> p b r c", b=B, r=4)[:, :, 0:3, 3]
-                nc.vector.tensor_tensor(out=sq[:], in0=dv, in1=dv, op=ALU.mult)
-            elif step == 2:
-                nc.vector.tensor_reduce(out=ss[:], in_=sq[:], axis=AX.X, op=ALU.add)
-            elif step == 3:
-                nc.gpsimd.tensor_tensor(out=base[:], in0=ss[:], in1=half[:], op=ALU.pow)
-            elif step == 4:
-                nc.vector.scalar_tensor_tensor(
-                    out=kk[:], in0=base[:], scalar=float(W), in1=fx[:], op0=ALU.mult, op1=ALU.mult
-                )
+        def camera_squares():
+            nc.gpsimd.tensor_tensor(out=dd[:], in0=ex1[:], in1=ex2[:], op=ALU.subtract)
+            dv = dd[:].rearrange("p (b r c) -> p b r c", b=B, r=4)[:, :, 0:3, 3]
+            nc.gpsimd.tensor_tensor(out=sq[:], in0=dv, in1=dv, op=ALU.mult)
+
+        def camera_factor():
+            nc.gpsimd.tensor_tensor(out=ss[:], in0=sq[:, :, 0], in1=sq[:, :, 1], op=ALU.add)
+            nc.gpsimd.tensor_tensor(out=ss[:], in0=ss[:], in1=sq[:, :, 2], op=ALU.add)
+            nc.gpsimd.tensor_tensor(out=base[:], in0=ss[:], in1=half[:], op=ALU.pow)
+            nc.gpsimd.tensor_scalar(
+                out=wb[:], in0=base[:], scalar1=float(W), scalar2=0.0, op0=ALU.mult, op1=ALU.add
+            )
+            nc.gpsimd.tensor_tensor(
+                out=kk[:], in0=wb[:], in1=in1[:].rearrange("p (b k) -> p b k", b=B)[:, :, 0], op=ALU.mult
+            )
 
         NC = N_UNITS * NT
         hc = NC // B
@@ -372,10 +387,22 @@ def tile_costvolume_kernel(tc, img1, img2, intri1, intri2, extri1, extri2, out_0
         def cols(b):
             return slice(hc * b, hc * (b + 1))
 
-        def f_cap(b):
-            view = bm_all[:].rearrange("p u (t s) -> p (u t) s", s=NK + NQD)[:, cols(b), 0:NQD]
+        diag_blocks = bm_all[:].rearrange("p u (t s) -> p (u t) s", s=NK + NQD)[:, :, 0:NQD]
+
+        def g_cap(u0, u1):
+            for k in range(NQD):
+                view = diag_blocks[:, NT * u0 : NT * u1, k]
+                nc.gpsimd.tensor_scalar(
+                    out=view, in0=view, scalar1=cap[:, k : k + 1], scalar2=-BIG, op0=ALU.min, op1=ALU.max
+                )
+
+        def v_cap(u0, u1):
+            view = diag_blocks[:, NT * u0 : NT * u1, :]
             nc.vector.tensor_tensor(
-                out=view, in0=view, in1=cap[:].unsqueeze(1).to_broadcast([P, hc, NQD]), op=ALU.min
+                out=view,
+                in0=view,
+                in1=cap[:].unsqueeze(1).to_broadcast([P, NT * (u1 - u0), NQD]),
+                op=ALU.min,
             )
 
         def f_pm(t, b):
@@ -465,7 +492,7 @@ def tile_costvolume_kernel(tc, img1, img2, intri1, intri2, extri1, extri2, out_0
             nc.gpsimd.tensor_tensor(out=conf[:, cols(0)], in0=cn[:, cols(0)], in1=rs[:, cols(0)], op=ALU.mult)
 
         early = {
-            19: [lambda: f_cap(0)],
+            19: [lambda: v_cap(0, hu)],
             20: [lambda: f_sc(0), lambda: f_pm(3, 0)],
             21: [lambda: f_rs(0), lambda: f_pm(2, 0)],
             22: [lambda: f_pm(1, 0)],
@@ -474,9 +501,9 @@ def tile_costvolume_kernel(tc, img1, img2, intri1, intri2, extri1, extri2, out_0
             25: [lambda: f_pe(0)],
             26: [lambda: f_cn(0)],
             28: [g_t1, g_df, g_conf],
-            29: [s_ab],
-            30: [lambda: f_den(0)],
-            31: [lambda: f_rd(0), g_depth],
+            29: [s_ab, camera_squares],
+            30: [lambda: f_den(0), camera_factor],
+            31: [lambda: g_cap(hu, last), lambda: f_rd(0), g_depth],
         }
         last = N_UNITS - 1
 
@@ -499,6 +526,8 @@ def tile_costvolume_kernel(tc, img1, img2, intri1, intri2, extri1, extri2, out_0
                 diag_max(i - 2 - BATCH, i - 2)
             if i >= 0:
                 row_max(i, [3, 2])
+            if r >= N_UNITS:
+                products(i - 1)
             if i - 1 >= 0:
                 weighted_sums(i - 1, [1])
             if i >= 0:
@@ -528,7 +557,10 @@ def tile_costvolume_kernel(tc, img1, img2, intri1, intri2, extri1, extri2, out_0
                     copy_passed(r - 1)
                 if r - 1 < N_UNITS:
                     regroup_part("s", r - 1, W, 2 * W - PW)
-            if i - 1 >= 0:
+            if r >= N_UNITS:
+                add_up(i - 1)
+                weighted_sums(i - 1, [3])
+            elif i - 1 >= 0:
                 weighted_sums(i - 1, [3, 0])
             if i == -1:
                 late_tables()
@@ -536,14 +568,14 @@ def tile_costvolume_kernel(tc, img1, img2, intri1, intri2, extri1, extri2, out_0
                 regroup_first(r)
             if i < 0 <= r - 1:
                 regroup_rest(r - 1)
+            if r - 1 == 1:
+                tables_to_sbuf()
             if i - 1 >= 0:
                 realign(i - 1)
             if i - 2 >= 0:
                 mask_diag(i - 2)
             if i == 2:
                 load_cameras()
-            if 8 <= i < 13:
-                camera(i - 8)
             for step in early.get(i, []):
                 step()
 
@@ -555,7 +587,7 @@ def tile_costvolume_kernel(tc, img1, img2, intri1, intri2, extri1, extri2, out_0
         weighted_sums(last, [1])
         f_sc(1)
         weighted_sums(last, [0])
-        f_cap(1)
+        v_cap(last, N_UNITS)
         f_df(1)
         f_pm(3, 1)
         f_ab(1)

@@ -31,12 +31,16 @@ SUM_CAP = 1.0e30
 FLOPS = 2 * B * H * W * W * C
 
 CV = 0
-HEAD = [[("s", 0, 160), ("v", 160, 896), ("s", 896, 1024)], [("v", 0, 512), ("s", 512, 832)], [("g", 0, 408), ("s", 408, 512)]]
 CG = 408
 PIN = True
 AHEAD = 4
 BATCH = 4
-PW = 192
+PW = 208
+HEAD = [
+    [("s", 0, 160), ("v", 160, 896), ("s", 896, 1024)],
+    [("v", 0, 512), ("s", 512, 2 * W - PW)],
+    [("g", 0, 408), ("s", 408, 512)],
+]
 
 
 def tile_costvolume_kernel(tc, img1, img2, intri1, intri2, extri1, extri2, out_0, out_1):
@@ -160,8 +164,9 @@ def tile_costvolume_kernel(tc, img1, img2, intri1, intri2, extri1, extri2, out_0
                 z = min(hi, W * (g + 1)) - W * g
                 if a >= z:
                     continue
-                src = raw[(g, u)][:, :, a:z].rearrange("p t (c i) -> p c t i", i=4)
-                dst = grouped[u][:, g, a:z, :].rearrange("p (c i) t -> p c t i", i=4)
+                run = 8 if kind == "s" else 4
+                src = raw[(g, u)][:, :, a:z].rearrange("p t (c i) -> p c t i", i=run)
+                dst = grouped[u][:, g, a:z, :].rearrange("p (c i) t -> p c t i", i=run)
                 if kind == "g":
                     src = raw[(g, u)][:, :, a:z].rearrange("p t w -> p w t")
                     dst = grouped[u][:, g, a:z, :]

from contextlib import ExitStack
import math

import concourse.bass as bass
import concourse.mybir as mybir
import concourse.tile as tile
from concourse.masks import make_identity

F32 = mybir.dt.float32
BF16 = mybir.dt.bfloat16
U32 = mybir.dt.uint32
U8 = mybir.dt.uint8
FP8X4 = mybir.dt.float8_e4m3fn_x4
ALU = mybir.AluOpType
ACT = mybir.ActivationFunctionType
AX = mybir.AxisListType

B, C, H, W = 2, 512, 16, 512
P = 128
PACK = 4
NT = W // P
N_UNITS = B * H
QUAD = 32
NK = W // QUAD
NQD = P // QUAD
LOOKAHEAD = 5
ORDER = (3, 2, 1, 0)
SCALE = 1.0 / math.sqrt(C)
BIG = 3.0e38
SUM_CAP = 1.0e30
FLOPS = 2 * B * H * W * W * C

CV = 0
CG = 408
PIN = True
AHEAD = 4
BATCH = 4
PW = 208
HEAD = [
    [("s", 0, 160), ("v", 160, 896), ("s", 896, 1024)],
    [("v", 0, 512), ("s", 512, 2 * W - PW)],
    [("g", 0, 408), ("s", 408, 512)],
]


def tile_costvolume_kernel(tc, img1, img2, intri1, intri2, extri1, extri2, out_0, out_1):
    nc = tc.nc
    with ExitStack() as ctx:
        const = ctx.enter_context(tc.tile_pool(name="const", bufs=1))
        rawp = ctx.enter_context(tc.tile_pool(name="rawp", bufs=LOOKAHEAD + 2))
        grpp = ctx.enter_context(tc.tile_pool(name="grpp", bufs=3))
        qp = ctx.enter_context(tc.tile_pool(name="qp", bufs=3))
        ep = ctx.enter_context(tc.tile_pool(name="ep", bufs=3))
        psum = ctx.enter_context(tc.psum_pool(name="psum", bufs=4))
        psp = ctx.enter_context(tc.psum_pool(name="psp", bufs=1))
        pst = ctx.enter_context(tc.psum_pool(name="pst", bufs=1))
        if PIN:
            ctx.enter_context(tc.manual_schedule())

        views = [im.rearrange("b (p j) h w -> b p j h w", j=PACK) for im in (img1, img2)]
        raw = {}
        grouped = {}
        codes = {}
        scales = {}
        banks = {}
        etile = {}
        passed = {}

        def load(q):
            for g in (0, 1):
                r = rawp.tile([P, PACK, W], BF16, tag="raw%d" % g, name="raw%d_%d" % (g, q))
                nc.sync.dma_start(out=r[:], in_=views[g][q // H, :, :, q % H, :])
                raw[(g, q)] = r

        for q in range(LOOKAHEAD):
            load(q)

        in1 = const.tile([P, 18], BF16, name="in1")
        ex1 = const.tile([P, 32], BF16, name="ex1")
        ex2 = const.tile([P, 32], BF16, name="ex2")

        def load_cameras():
            for dst, src in ((in1, intri1), (ex1, extri1), (ex2, extri2)):
                nc.sync.dma_start(out=dst[:], in_=src.rearrange("b r c -> (b r c)").partition_broadcast(P))

        warm = const.tile([P, 1], F32, name="warm")
        warm2 = const.tile([P, 1], F32, name="warm2")
        nc.vector.memset(warm[:], 0.0)
        nc.scalar.activation(out=warm2[:], in_=warm[:], func=ACT.Exp)

        ident_bf = const.tile([P, P], BF16, name="ident_bf")
        make_identity(nc, ident_bf[:])
        ident = const.tile([P, P], F32, name="ident")
        make_identity(nc, ident[:])
        column_w = const.tile([P, NT, P], F32, name="column_w")
        diag_w = const.tile([P, NT, P], F32, name="diag_w")
        nc.gpsimd.iota(
            column_w[:], pattern=[[P, NT], [0, P]], base=0, channel_multiplier=1, allow_small_or_imprecise_dtypes=True
        )
        nc.gpsimd.affine_select(
            out=diag_w[:],
            in_=column_w[:],
            pattern=[[0, NT], [1, P]],
            compare_op=ALU.is_ge,
            fill=0.0,
            base=0,
            channel_multiplier=-1,
        )
        bigt = const.tile([P, NQD], F32, name="bigt")
        cap = const.tile([P, NQD], F32, name="cap")
        nc.vector.memset(bigt[:], BIG)
        ones = const.tile([P, QUAD], F32, name="ones")
        tril = const.tile([P, QUAD], F32, name="tril")
        nc.vector.memset(ones[:], 1.0)
        half = const.tile([P, B], F32, name="half")
        w1_f = const.tile([P, P], F32, name="w1_f")

        def late_tables():
            for qd in range(NQD):
                nc.gpsimd.affine_select(
                    out=tril[QUAD * qd : QUAD * (qd + 1), :],
                    in_=ones[QUAD * qd : QUAD * (qd + 1), :],
                    pattern=[[-1, QUAD]],
                    compare_op=ALU.is_ge,
                    fill=0.0,
                    base=0,
                    channel_multiplier=1,
                )
            nc.gpsimd.affine_select(
                out=cap[:],
                in_=bigt[:],
                pattern=[[-QUAD, NQD]],
                compare_op=ALU.is_ge,
                fill=-BIG,
                base=-QUAD,
                channel_multiplier=1,
            )
            nc.gpsimd.memset(half[:], 0.5)
            nc.gpsimd.iota(
                w1_f[:],
                pattern=[[0, N_UNITS], [P, NT]],
                base=0,
                channel_multiplier=1,
                allow_small_or_imprecise_dtypes=True,
            )

        bm_all = const.tile([P, N_UNITS, NT * (NK + NQD)], F32, name="bm_all")
        for t in range(NT - 1):
            unused = bm_all[:, :, 0 : NT * NK].rearrange("p u (t k) -> p u t k", k=NK)[:, :, t, NQD * (t + 1) : NK]
            nc.vector.memset(unused, -BIG)
        m_all = const.tile([P, N_UNITS * NT], F32, name="m_all")
        bias_all = const.tile([P, N_UNITS * NT], F32, name="bias_all")
        sums = const.tile([P, N_UNITS * NT], F32, name="sums")
        num_all = const.tile([P, N_UNITS * NT], F32, name="num_all")
        dmax_all = const.tile([P, N_UNITS * NT], F32, name="dmax_all")
        draw_all = const.tile([P, N_UNITS, NT, QUAD], F32, name="draw_all")
        dm_all = const.tile([P, N_UNITS, NT, QUAD], F32, name="dm_all")
        offs = [P * t * (t + 1) // 2 for t in range(NT)]
        junk = [const.tile([P, P * NT * (NT + 1) // 2], F32, name="junk%d" % k) for k in range(2)]

        def regroup_part(kind, u, lo, hi):
            for g in (0, 1):
                a = max(lo, W * g) - W * g
                z = min(hi, W * (g + 1)) - W * g
                if a >= z:
                    continue
                run = 8 if kind == "s" else 4
                src = raw[(g, u)][:, :, a:z].rearrange("p t (c i) -> p c t i", i=run)
                dst = grouped[u][:, g, a:z, :].rearrange("p (c i) t -> p c t i", i=run)
                if kind == "g":
                    src = raw[(g, u)][:, :, a:z].rearrange("p t w -> p w t")
                    dst = grouped[u][:, g, a:z, :]
                if kind == "v":
                    nc.vector.tensor_copy(out=dst, in_=src)
                elif kind == "s":
                    nc.scalar.copy(out=dst, in_=src)
                else:
                    nc.gpsimd.tensor_scalar(out=dst, in0=src, scalar1=1.0, scalar2=0.0, op0=ALU.mult, op1=ALU.add)

        def pass_through(u):
            pt = psp.tile([P, 2 * W], BF16, tag="pt", name="pt_%d" % u)
            passed[u] = pt
            for lo, hi in ((0, P), (P, PW)):
                nc.tensor.matmul(
                    out=pt[:, PACK * lo : PACK * hi],
                    lhsT=ident_bf[:],
                    rhs=raw[(1, u)][:, :, W - PW + lo : W - PW + hi].rearrange("p t w -> p w t"),
                    start=True,
                    stop=True,
                )

        def shares(u):
            if u < len(HEAD):
                return HEAD[u]
            return [("g", 0, CG), ("v", CG, CG + CV), ("s", CG + CV, 2 * W - PW)]

        def regroup_first(u):
            grouped[u] = grpp.tile([P, 2, W, PACK], BF16, tag="grouped", name="grouped_%d" % u, align_bytes=64)
            for kind, lo, hi in shares(u):
                if kind == "g":
                    regroup_part(kind, u, lo, hi)

        def regroup_rest(u):
            for kind, lo, hi in shares(u):
                if kind != "g":
                    regroup_part(kind, u, lo, hi)
            if u == 1:
                copy_passed(u)

        def copy_passed(u):
            nc.scalar.copy(
                out=grouped[u][:, 1, W - PW : W, :].rearrange("p w t -> p (w t)"), in_=passed[u][:, 0 : PACK * PW]
            )

        def quantise(u):
            codes[u] = qp.tile([P, 2 * W], U32, tag="codes", name="codes_%d" % u, align_bytes=64)
            scales[u] = qp.tile([P, 2 * W], U8, tag="scales", name="scales_%d" % u, align_bytes=64)
            nc.vector.quantize_mx(
                out=codes[u][:].bitcast(FP8X4),
                scales=scales[u][:],
                in_=grouped[u][:].rearrange("p g w j -> p (g w j)"),
            )

        def multiply(u, tiles):
            for t in tiles:
                bank = psum.tile([P, W], F32, tag="bank", name="bank_%d_%d" % (u, t))
                banks[(u, t)] = bank
                nc.tensor.matmul_mx(
                    out=bank[:],
                    lhsT=codes[u][:, P * t : P * (t + 1)].bitcast(FP8X4),
                    lhsT_scale=scales[u][:, P * t : P * (t + 1)],
                    rhs=codes[u][:, W : 2 * W].bitcast(FP8X4),
                    rhs_scale=scales[u][:, W : 2 * W],
                    start=True,
                    stop=True,
                )

        def row_max(u, tiles):
            for t in tiles:
                nc.vector.tensor_reduce(
                    out=bm_all[:, u, NK * t : NK * t + NQD * (t + 1)],
                    in_=banks[(u, t)][:, 0 : P * (t + 1)].rearrange("p (k r) -> p k r", r=QUAD),
                    axis=AX.X,
                    op=ALU.max,
                )

        def row_max_pair(u, pair):
            lo = 2 * pair
            nc.vector.tensor_reduce(
                out=m_all[:, NT * u + lo : NT * u + lo + 2],
                in_=bm_all[:, u, NK * lo : NK * (lo + 2)].rearrange("p (t k) -> p t k", k=NK),
                axis=AX.X,
                op=ALU.max,
            )

        def biases(u, pair):
            c0 = NT * u + 2 * pair
            nc.scalar.mul(out=bias_all[:, c0 : c0 + 2], in_=m_all[:, c0 : c0 + 2], mul=-SCALE)

        def exponentials(u, pair):
            if pair == 1:
                etile[u] = ep.tile([P, NT * (W + P)], F32, tag="e", name="e_%d" % u)
            for t in (2 * pair + 1, 2 * pair):
                col = NT * u + t
                nc.scalar.activation(
                    out=etile[u][:, W * t : W * (t + 1)],
                    in_=banks[(u, t)][:],
                    func=ACT.Exp,
                    bias=bias_all[:, col : col + 1],
                    scale=SCALE,
                    accum_out=sums[:, col : col + 1],
                )

        def realign(u):
            for qd in range(NQD):
                rows = slice(QUAD * qd, QUAD * (qd + 1))
                nc.sync.dma_start(
                    out=draw_all[rows, u, :, :],
                    in_=etile[u][rows, :].rearrange("p (t s) -> p t s", s=W + P)[:, :, QUAD * qd : QUAD * (qd + 1)],
                )

        def mask_diag(u):
            nc.gpsimd.tensor_tensor(
                out=dm_all[:, u, :, :],
                in0=draw_all[:, u, :, :],
                in1=tril[:].unsqueeze(1).to_broadcast([P, NT, QUAD]),
                op=ALU.mult,
            )

        tab_a = pst.tile([P, W], F32, tag="tab_a", name="tab_a")
        tab_b = pst.tile([P, W], F32, tag="tab_b", name="tab_b")
        tab_c = pst.tile([P, W], F32, tag="tab_c", name="tab_c")
        weights = {
            0: tab_b[:, 3 * P : 4 * P],
            1: tab_c[:, 0 : 2 * P],
            2: tab_b[:, 0 : 3 * P],
            3: tab_a[:, 0 : 4 * P],
        }

        def tables_to_psum():
            for t in range(NT):
                for c in range(t + 1):
                    src = diag_w if c == t else column_w
                    nc.tensor.transpose(out=weights[t][:, P * c : P * (c + 1)], in_=src[:, c, :], identity=ident[:])

        def weighted_sums(u, tiles):
            for t in tiles:
                n = P * (t + 1)
                col = NT * u + t
                nc.vector.scalar_tensor_tensor(
                    out=junk[u % 2][:, offs[t] : offs[t] + n],
                    in0=etile[u][:, W * t : W * t + n],
                    scalar=1.0,
                    in1=weights[t],
                    op0=ALU.mult,
                    op1=ALU.mult,
                    accum_out=num_all[:, col : col + 1],
                )

        weights_sb = const.tile([P, P], F32, name="weights_sb")
        prod = [const.tile([P, P], F32, name="prod%d" % k) for k in range(2)]
        summed = const.tile([P, P], F32, name="summed")

        def tables_to_sbuf():
            nc.scalar.copy(out=weights_sb[:], in_=weights[0])

        def products(u):
            nc.gpsimd.tensor_tensor(out=prod[u % 2][:], in0=etile[u][:, 0:P], in1=weights_sb[:], op=ALU.mult)

        def add_up(u):
            nc.scalar.activation(
                out=summed[:], in_=prod[u % 2][:], func=ACT.Copy, accum_out=num_all[:, NT * u : NT * u + 1]
            )

        def mask_diag_direct(u, qd):
            rows = slice(QUAD * qd, QUAD * (qd + 1))
            nc.gpsimd.tensor_tensor(
                out=dm_all[rows, u, :, :],
                in0=etile[u][rows, :].rearrange("p (t s) -> p t s", s=W + P)[:, :, QUAD * qd : QUAD * (qd + 1)],
                in1=tril[rows, :].unsqueeze(1).to_broadcast([QUAD, NT, QUAD]),
                op=ALU.mult,
            )

        def diag_max(u0, u1):
            nc.vector.tensor_reduce(
                out=dmax_all[:, NT * u0 : NT * u1],
                in_=dm_all[:, u0:u1, :, :].rearrange("p u t r -> p (u t) r"),
                axis=AX.X,
                op=ALU.max,
            )

        dd = const.tile([P, 32], F32, name="dd")
        sq = const.tile([P, B, 3], F32, name="sq")
        ss = const.tile([P, B], F32, name="ss")
        base = const.tile([P, B], F32, name="base")
        wb = const.tile([P, B], F32, name="wb")
        kk = const.tile([P, B], F32, name="kk")

        def camera_squares():
            nc.gpsimd.tensor_tensor(out=dd[:], in0=ex1[:], in1=ex2[:], op=ALU.subtract)
            dv = dd[:].rearrange("p (b r c) -> p b r c", b=B, r=4)[:, :, 0:3, 3]
            nc.gpsimd.tensor_tensor(out=sq[:], in0=dv, in1=dv, op=ALU.mult)

        def camera_factor():
            nc.gpsimd.tensor_tensor(out=ss[:], in0=sq[:, :, 0], in1=sq[:, :, 1], op=ALU.add)
            nc.gpsimd.tensor_tensor(out=ss[:], in0=ss[:], in1=sq[:, :, 2], op=ALU.add)
            nc.gpsimd.tensor_tensor(out=base[:], in0=ss[:], in1=half[:], op=ALU.pow)
            nc.gpsimd.tensor_scalar(
                out=wb[:], in0=base[:], scalar1=float(W), scalar2=0.0, op0=ALU.mult, op1=ALU.add
            )
            nc.gpsimd.tensor_tensor(
                out=kk[:], in0=wb[:], in1=in1[:].rearrange("p (b k) -> p b k", b=B)[:, :, 0], op=ALU.mult
            )

        NC = N_UNITS * NT
        hc = NC // B
        hu = N_UNITS // B
        pm = const.tile([P, NC], F32, name="pm")
        arg = const.tile([P, NC], F32, name="arg")
        pe = const.tile([P, NC], F32, name="pe")
        sc = const.tile([P, NC], F32, name="sc")
        rs = const.tile([P, NC], F32, name="rs")
        t1 = const.tile([P, NC], F32, name="t1")
        df = const.tile([P, NC], F32, name="df")
        ab = const.tile([P, NC], F32, name="ab")
        den = const.tile([P, NC], F32, name="den")
        rd = const.tile([P, NC], F32, name="rd")
        depth = const.tile([P, NC], F32, name="depth")
        cn = const.tile([P, NC], F32, name="cn")
        conf = const.tile([P, NC], F32, name="conf")

        def cols(b):
            return slice(hc * b, hc * (b + 1))

        diag_blocks = bm_all[:].rearrange("p u (t s) -> p (u t) s", s=NK + NQD)[:, :, 0:NQD]

        def g_cap(u0, u1):
            for k in range(NQD):
                view = diag_blocks[:, NT * u0 : NT * u1, k]
                nc.gpsimd.tensor_scalar(
                    out=view, in0=view, scalar1=cap[:, k : k + 1], scalar2=-BIG, op0=ALU.min, op1=ALU.max
                )

        def v_cap(u0, u1):
            view = diag_blocks[:, NT * u0 : NT * u1, :]
            nc.vector.tensor_tensor(
                out=view,
                in0=view,
                in1=cap[:].unsqueeze(1).to_broadcast([P, NT * (u1 - u0), NQD]),
                op=ALU.min,
            )

        def f_pm(t, b):
            nc.vector.tensor_reduce(
                out=pm[:].rearrange("p (u t) -> p u t", t=NT)[:, hu * b : hu * (b + 1), t],
                in_=bm_all[:, hu * b : hu * (b + 1), NK * t : NK * t + NQD * (t + 1)],
                axis=AX.X,
                op=ALU.max,
            )

        def f_arg(b):
            nc.vector.scalar_tensor_tensor(
                out=arg[:, cols(b)], in0=pm[:, cols(b)], scalar=SCALE, in1=bias_all[:, cols(b)], op0=ALU.mult, op1=ALU.add
            )

        def f_pe(b):
            nc.scalar.activation(out=pe[:, cols(b)], in_=arg[:, cols(b)], func=ACT.Exp)

        def f_sc(b):
            nc.vector.tensor_scalar(
                out=sc[:, cols(b)], in0=sums[:, cols(b)], scalar1=SUM_CAP, scalar2=None, op0=ALU.min
            )

        def f_rs(b):
            nc.vector.reciprocal(out=rs[:, cols(b)], in_=sc[:, cols(b)])

        def f_t1(b):
            nc.vector.scalar_tensor_tensor(
                out=t1[:, cols(b)],
                in0=sums[:, cols(b)],
                scalar=SUM_CAP,
                in1=w1_f[:, cols(b)],
                op0=ALU.min,
                op1=ALU.mult,
            )

        def f_df(b):
            nc.vector.tensor_tensor(out=df[:, cols(b)], in0=num_all[:, cols(b)], in1=t1[:, cols(b)], op=ALU.subtract)

        def f_ab(b):
            nc.vector.scalar_tensor_tensor(
                out=ab[:, cols(b)], in0=df[:, cols(b)], scalar=-1.0, in1=df[:, cols(b)], op0=ALU.mult, op1=ALU.max
            )

        def f_den(b):
            nc.vector.scalar_tensor_tensor(
                out=den[:, cols(b)], in0=sc[:, cols(b)], scalar=0.1 * W, in1=ab[:, cols(b)], op0=ALU.mult, op1=ALU.max
            )

        def f_rd(b):
            nc.vector.reciprocal(out=rd[:, cols(b)], in_=den[:, cols(b)])

        def f_depth(b):
            nc.vector.scalar_tensor_tensor(
                out=depth[:, cols(b)],
                in0=rd[:, cols(b)],
                scalar=kk[:, b : b + 1],
                in1=sc[:, cols(b)],
                op0=ALU.mult,
                op1=ALU.mult,
            )

        def f_cn(b):
            nc.vector.tensor_tensor(out=cn[:, cols(b)], in0=pe[:, cols(b)], in1=dmax_all[:, cols(b)], op=ALU.max)

        def f_conf(b):
            nc.vector.tensor_tensor(out=conf[:, cols(b)], in0=cn[:, cols(b)], in1=rs[:, cols(b)], op=ALU.mult)

        dq = const.tile([P, hc], F32, name="dq")

        def g_t1():
            nc.gpsimd.tensor_tensor(out=t1[:, cols(0)], in0=sc[:, cols(0)], in1=w1_f[:, cols(0)], op=ALU.mult)

        def g_df():
            nc.gpsimd.tensor_tensor(out=df[:, cols(0)], in0=num_all[:, cols(0)], in1=t1[:, cols(0)], op=ALU.subtract)

        def s_ab():
            nc.scalar.activation(out=ab[:, cols(0)], in_=df[:, cols(0)], func=ACT.Abs)

        def g_depth():
            nc.gpsimd.tensor_tensor(out=dq[:], in0=rd[:, cols(0)], in1=sc[:, cols(0)], op=ALU.mult)
            nc.gpsimd.tensor_scalar(
                out=depth[:, cols(0)], in0=dq[:], scalar1=kk[:, 0:1], scalar2=0.0, op0=ALU.mult, op1=ALU.add
            )

        def g_conf():
            nc.gpsimd.tensor_tensor(out=conf[:, cols(0)], in0=cn[:, cols(0)], in1=rs[:, cols(0)], op=ALU.mult)

        early = {
            19: [lambda: v_cap(0, hu)],
            20: [lambda: f_sc(0), lambda: f_pm(3, 0)],
            21: [lambda: f_rs(0), lambda: f_pm(2, 0)],
            22: [lambda: f_pm(1, 0)],
            23: [lambda: f_pm(0, 0)],
            24: [lambda: f_arg(0)],
            25: [lambda: f_pe(0)],
            26: [lambda: f_cn(0)],
            28: [g_t1, g_df, g_conf],
            29: [s_ab, camera_squares],
            30: [lambda: f_den(0), camera_factor],
            31: [lambda: g_cap(hu, last), lambda: f_rd(0), g_depth],
        }
        last = N_UNITS - 1

        for i in range(-AHEAD, N_UNITS):
            r = i + AHEAD
            if r + LOOKAHEAD < N_UNITS:
                load(r + LOOKAHEAD)
            if 2 <= i + 1 < N_UNITS:
                quantise(i + 1)
            if 1 <= r - 1 < N_UNITS and i != 0:
                pass_through(r - 1)
            if r - 1 == 0:
                tables_to_psum()
            if 2 <= i + 1 < N_UNITS:
                multiply(i + 1, ORDER)
            if r - 1 == 1:
                quantise(0)
                multiply(0, ORDER)
            if i - 3 >= 0 and (i - 3) % BATCH == BATCH - 1:
                diag_max(i - 2 - BATCH, i - 2)
            if i >= 0:
                row_max(i, [3, 2])
            if r >= N_UNITS:
                products(i - 1)
            if i - 1 >= 0:
                weighted_sums(i - 1, [1])
            if i >= 0:
                row_max_pair(i, 1)
                biases(i, 1)
                if i == 0:
                    copy_passed(2)
                    pass_through(3)
                elif r - 1 < N_UNITS:
                    regroup_part("s", r - 1, CG + CV, W)
                exponentials(i, 1)
                row_max(i, [1, 0])
            if i - 1 >= 0:
                weighted_sums(i - 1, [2])
            if i >= 0:
                row_max_pair(i, 0)
                biases(i, 0)
                if i == 0:
                    quantise(1)
                    multiply(1, ORDER)
                    regroup_part("v", 2, W, 2 * W - PW)
                    regroup_part("s", r - 1, CG + CV, W)
                elif r - 1 < N_UNITS:
                    copy_passed(r - 1)
                exponentials(i, 0)
                if i == 0:
                    copy_passed(r - 1)
                if r - 1 < N_UNITS:
                    regroup_part("s", r - 1, W, 2 * W - PW)
            if r >= N_UNITS:
                add_up(i - 1)
                weighted_sums(i - 1, [3])
            elif i - 1 >= 0:
                weighted_sums(i - 1, [3, 0])
            if i == -1:
                late_tables()
            if r < N_UNITS:
                regroup_first(r)
            if i < 0 <= r - 1:
                regroup_rest(r - 1)
            if r - 1 == 1:
                tables_to_sbuf()
            if i - 1 >= 0:
                realign(i - 1)
            if i - 2 >= 0:
                mask_diag(i - 2)
            if i == 2:
                load_cameras()
            for step in early.get(i, []):
                step()

        mask_diag(last - 1)
        for qd in range(NQD):
            mask_diag_direct(last, qd)
        weighted_sums(last, [3, 2])
        f_t1(1)
        weighted_sums(last, [1])
        f_sc(1)
        weighted_sums(last, [0])
        v_cap(last, N_UNITS)
        f_df(1)
        f_pm(3, 1)
        f_ab(1)
        f_pm(2, 1)
        f_den(1)
        f_pm(1, 1)
        f_pm(0, 1)
        f_rd(1)
        f_rs(1)
        f_arg(1)
        f_pe(1)
        f_depth(1)
        diag_max(N_UNITS - BATCH, N_UNITS)
        f_cn(1)
        f_conf(1)

        pt0 = psum.tile([P, W], F32, tag="bank", name="pt0")
        pt1 = psum.tile([P, W], F32, tag="bank", name="pt1")
        o0 = const.tile([P, P], F32, name="o0")
        o1 = const.tile([P, P], F32, name="o1")
        nc.tensor.transpose(out=pt0[:, 0:P], in_=depth[:], identity=ident[:])
        nc.scalar.copy(out=o0[:], in_=pt0[:, 0:P])
        nc.sync.dma_start(out=out_0.rearrange("b o h (t p) -> (b o h t) p", p=P), in_=o0[:])
        nc.tensor.transpose(out=pt1[:, 0:P], in_=conf[:], identity=ident[:])
        nc.scalar.copy(out=o1[:], in_=pt1[:, 0:P])
        nc.scalar.dma_start(out=out_1.rearrange("b o h (t p) -> (b o h t) p", p=P), in_=o1[:])
